import numpy as np
import ml_dtypes


def mxq(x, axis, fmt="e4m3"):
    dtype, down = {"e4m3": (ml_dtypes.float8_e4m3fn, 7), "e5m2": (ml_dtypes.float8_e5m2, 14)}[fmt]
    v = np.moveaxis(np.asarray(x, np.float32).astype(ml_dtypes.bfloat16).astype(np.float64), axis, -1)
    blocks = v.reshape(v.shape[:-1] + (-1, 32))
    amax = np.abs(blocks).max(-1, keepdims=True)
    byte = np.maximum(np.where(amax > 0, np.frexp(amax)[1] - 1 + 127, 0) - down, 1)
    scale = np.exp2(byte - 127.0)
    codes = (blocks / scale).astype(np.float32).astype(dtype).astype(np.float64)
    return np.moveaxis((codes * scale).reshape(v.shape), -1, axis)


WIDE = False


def mx_kscale(k):
    if not WIDE:
        return np.ones(k)
    levels = np.array([10, -10, 5, -5, 0])
    a = np.random.permutation(np.resize(levels, k // 512 * 4)).reshape(k // 512, 4)
    idx = np.arange(k)
    return np.exp2(a[idx // 512, idx % 128 // 32])


BF16 = ml_dtypes.bfloat16


def bf(x):
    return np.asarray(x, np.float32).astype(BF16)


def f64(x):
    return np.asarray(x).astype(np.float64)


B, M, D, N, P, H = 4, 128, 512, 4, 8, 512
R = B * P


def silu(v):
    return v / (1.0 + np.exp(-v))


def setup_inputs():
    s = mx_kscale(D)
    return {"xs_mix": bf(np.random.standard_normal((B, N, P, D)) * 0.3 / np.sqrt(D) * s),
            "task_emb": bf(np.random.standard_normal((P, D)) * 0.5 / np.sqrt(D) * s),
            "W1": bf(np.random.standard_normal((N, D, H)) * 2.0 / s[:, None]),
            "b1": bf(np.random.standard_normal((N, H)) * 0.3),
            "W2": bf(np.random.standard_normal((N, H, D)) / np.sqrt(H * D) * s),
            "b2": bf(np.random.standard_normal((N, D)) * 0.3 / np.sqrt(D) * s),
            "ln_g": bf(1.0 + 0.1 * np.random.standard_normal((N, D))),
            "ln_b": bf(0.1 * np.random.standard_normal((N, D)))}


def reference(xs_mix, task_emb, W1, b1, W2, b2, ln_g, ln_b):
    xs = f64(xs_mix) + f64(task_emb)[None, None, :, :]
    xe = xs.transpose(1, 0, 2, 3).reshape(N, R, D)
    h = silu((mxq(xe, 2, "e4m3") @ mxq(f64(W1), 1, "e4m3")) + f64(b1)[:, None, :])
    mlp = (mxq(h, 2, "e4m3") @ mxq(f64(W2), 1, "e4m3")) + f64(b2)[:, None, :]
    r = xe + mlp
    mu = r.mean(-1, keepdims=True)
    var = ((r - mu) ** 2).mean(-1, keepdims=True)
    ys = (r - mu) / np.sqrt(var + 1e-5) * f64(ln_g)[:, None, :] + f64(ln_b)[:, None, :]
    return ys.reshape(N, B, P, D).transpose(1, 0, 2, 3)

@@ -1,0 +1,234 @@
+import concourse.mybir as mybir
+from concourse.masks import make_identity
+
+F32 = mybir.dt.float32
+BF16 = mybir.dt.bfloat16
+U32 = mybir.dt.uint32
+U8 = mybir.dt.uint8
+FP8X4 = mybir.dt.float8_e4m3fn_x4
+ALU = mybir.AluOpType
+ACT = mybir.ActivationFunctionType
+
+P = 128
+PACK = 4
+BATCH = 4
+EXPERTS = 4
+TASKS = 8
+ROWS = BATCH * EXPERTS * TASKS
+WIDTH = 512
+CHUNKS = WIDTH // P
+EPS = 1e-5
+
+ROW_TASK = 0
+ROW_B1 = ROW_TASK + TASKS
+ROW_B2 = ROW_B1 + EXPERTS
+ROW_GAIN = ROW_B2 + EXPERTS
+ROW_SHIFT = ROW_GAIN + EXPERTS
+SMALL_ROWS = ROW_SHIFT + EXPERTS
+
+VECTOR_COLS = 256
+
+FLOPS = 2 * 2 * ROWS * WIDTH * WIDTH
+
+
+def regroup(engine_copy, grouped, raw, cols):
+    engine_copy(
+        out=grouped[:, cols, :].rearrange("q (c i) j -> q c j i", i=4),
+        in_=raw[:, :, cols].rearrange("q j (c i) -> q c j i", i=4),
+    )
+
+
+def tile_hdmodel_pb_s_kernel(tc, xs_mix, task_emb, W1, b1, W2, b2, ln_g, ln_b, out):
+    nc = tc.nc
+    with (
+        tc.tile_pool(name="keep", bufs=1) as keep,
+        tc.tile_pool(name="weights", bufs=2 * EXPERTS) as weights,
+        tc.tile_pool(name="stage", bufs=3) as stage,
+        tc.psum_pool(name="psum", bufs=1) as psum,
+        tc.psum_pool(name="psum_hidden", bufs=2) as psum_hidden,
+    ):
+        small = keep.tile([P, WIDTH], BF16)
+        nc.vector.memset(small[:], 0.0)
+        h_grouped = keep.tile([P, EXPERTS, ROWS, PACK], BF16, align_bytes=64)
+        nc.vector.memset(h_grouped[:], 0.0)
+        minus_half = keep.tile([P, 1], F32)
+        nc.vector.memset(minus_half[:], -0.5)
+        ident_bf = keep.tile([P, P], BF16)
+        make_identity(nc, ident_bf[:])
+        ident_f32 = keep.tile([P, P], F32)
+        make_identity(nc, ident_f32[:])
+
+        x_mix = keep.tile([ROWS, WIDTH], BF16)
+        nc.sync.dma_start(out=x_mix[:], in_=xs_mix.flatten_outer_dims())
+        nc.scalar.dma_start(out=small[ROW_TASK : ROW_TASK + TASKS, :], in_=task_emb)
+        nc.scalar.dma_start(out=small[ROW_B1 : ROW_B1 + EXPERTS, :], in_=b1)
+        nc.scalar.dma_start(out=small[ROW_B2 : ROW_B2 + EXPERTS, :], in_=b2)
+        nc.scalar.dma_start(out=small[ROW_GAIN : ROW_GAIN + EXPERTS, :], in_=ln_g)
+        nc.scalar.dma_start(out=small[ROW_SHIFT : ROW_SHIFT + EXPERTS, :], in_=ln_b)
+        raw_tiles = []
+        for n in range(EXPERTS):
+            raw = weights.tile([P, PACK, WIDTH], BF16)
+            nc.sync.dma_start(out=raw[:], in_=W1[n].rearrange("(q j) w -> q j w", j=PACK))
+            raw_tiles.append(raw)
+        for n in range(EXPERTS):
+            raw = weights.tile([P, PACK, WIDTH], BF16)
+            nc.sync.dma_start(out=raw[:], in_=W2[n].rearrange("(t q) w -> q t w", q=P))
+            raw_tiles.append(raw)
+
+        warm = keep.tile([P, 1], F32)
+        nc.scalar.activation(out=warm[:], in_=minus_half[:], func=ACT.Silu)
+
+        small_t_packed = psum.tile([P, PACK, P], BF16)
+        for j in range(PACK):
+            nc.tensor.transpose(
+                small_t_packed[:, j, :], small[:].rearrange("v (q j) -> v j q", j=PACK)[:, j, :], ident_bf[:]
+            )
+        task_t_packed = keep.tile([P, PACK, TASKS], BF16)
+        nc.vector.tensor_copy(out=task_t_packed[:], in_=small_t_packed[:, :, ROW_TASK : ROW_TASK + TASKS])
+        small_t_psum = psum.tile([P, CHUNKS, P], BF16)
+        for c in range(CHUNKS):
+            nc.tensor.transpose(small_t_psum[:, c, :], small[:, c * P : (c + 1) * P], ident_bf[:])
+        small_t = keep.tile([P, CHUNKS, SMALL_ROWS], BF16)
+        nc.vector.tensor_copy(out=small_t[:], in_=small_t_psum[:, :, 0:SMALL_ROWS])
+
+        x_t = psum.tile([P, PACK, ROWS], BF16)
+        for j in range(PACK):
+            nc.tensor.transpose(
+                x_t[:, j, :], x_mix[:].rearrange("r (q j) -> r j q", j=PACK)[:, j, :], ident_bf[:]
+            )
+        x_grouped = keep.tile([P, ROWS, PACK], BF16, align_bytes=64)
+        nc.vector.tensor_tensor(
+            out=x_grouped[:].rearrange("q (a p) j -> q a p j", p=TASKS),
+            in0=x_t[:].rearrange("q j (a p) -> q a p j", p=TASKS),
+            in1=task_t_packed[:]
+            .rearrange("q j p -> q p j")
+            .unsqueeze(1)
+            .to_broadcast([P, BATCH * EXPERTS, TASKS, PACK]),
+            op=ALU.add,
+        )
+        x_codes = keep.tile([P, ROWS], U32, align_bytes=64)
+        x_scales = keep.tile([P, ROWS], U8, align_bytes=64)
+        nc.vector.quantize_mx(
+            out=x_codes[:].bitcast(FP8X4),
+            scales=x_scales[:],
+            in_=x_grouped[:].rearrange("q r j -> q (r j)"),
+        )
+
+        h_codes = keep.tile([P, EXPERTS, ROWS], U32, align_bytes=64)
+        h_scales = keep.tile([P, EXPERTS, ROWS], U8, align_bytes=64)
+        result = psum.tile([ROWS, WIDTH], F32)
+        for layer in range(2):
+            for n in range(EXPERTS):
+                raw = raw_tiles[layer * EXPERTS + n]
+                grouped = stage.tile([P, WIDTH, PACK], BF16, align_bytes=64)
+                regroup(nc.vector.tensor_copy, grouped, raw, slice(0, VECTOR_COLS))
+                regroup(nc.scalar.copy, grouped, raw, slice(VECTOR_COLS, WIDTH))
+                w_codes = weights.tile([P, WIDTH], U32, align_bytes=64)
+                w_scales = weights.tile([P, WIDTH], U8, align_bytes=64)
+                nc.vector.quantize_mx(
+                    out=w_codes[:].bitcast(FP8X4),
+                    scales=w_scales[:],
+                    in_=grouped[:].rearrange("q w j -> q (w j)"),
+                )
+                if layer == 0:
+                    hidden = psum_hidden.tile([P, PACK, ROWS], F32)
+                    for t in range(PACK):
+                        nc.tensor.matmul_mx(
+                            out=hidden[:, t, :],
+                            lhsT=w_codes[:, t * P : (t + 1) * P].bitcast(FP8X4),
+                            lhsT_scale=w_scales[:, t * P : (t + 1) * P],
+                            rhs=x_codes[:].bitcast(FP8X4),
+                            rhs_scale=x_scales[:],
+                            start=True,
+                            stop=True,
+                        )
+                    biased = stage.tile([P, PACK, BATCH, TASKS], F32)
+                    nc.vector.tensor_tensor(
+                        out=biased[:],
+                        in0=hidden[:].rearrange("q t (b m p) -> q t b m p", b=BATCH, m=EXPERTS)[:, :, :, n, :],
+                        in1=small_t[:, :, ROW_B1 + n]
+                        .unsqueeze(2)
+                        .unsqueeze(3)
+                        .to_broadcast([P, PACK, BATCH, TASKS]),
+                        op=ALU.add,
+                    )
+                    nc.scalar.activation(
+                        out=h_grouped[:, n].rearrange("q (b m p) t -> q b m p t", b=BATCH, m=EXPERTS)[:, :, n, :, :],
+                        in_=biased[:].rearrange("q t b p -> q b p t"),
+                        func=ACT.Silu,
+                    )
+                    nc.vector.quantize_mx(
+                        out=h_codes[:, n, :].bitcast(FP8X4),
+                        scales=h_scales[:, n, :],
+                        in_=h_grouped[:, n].rearrange("q r t -> q (r t)"),
+                    )
+                else:
+                    nc.tensor.matmul_mx(
+                        out=result[:],
+                        lhsT=h_codes[:, n, :].bitcast(FP8X4),
+                        lhsT_scale=h_scales[:, n, :],
+                        rhs=w_codes[:].bitcast(FP8X4),
+                        rhs_scale=w_scales[:],
+                        start=(n == 0),
+                        stop=(n == EXPERTS - 1),
+                    )
+            if layer == 0:
+                add_np = keep.tile([P, CHUNKS, EXPERTS, TASKS], F32)
+                nc.vector.tensor_tensor(
+                    out=add_np[:],
+                    in0=small_t[:, :, ROW_B2 : ROW_B2 + EXPERTS].unsqueeze(3).to_broadcast([P, CHUNKS, EXPERTS, TASKS]),
+                    in1=small_t[:, :, ROW_TASK : ROW_TASK + TASKS].unsqueeze(2).to_broadcast([P, CHUNKS, EXPERTS, TASKS]),
+                    op=ALU.add,
+                )
+                add_t = keep.tile([P, CHUNKS, BATCH, EXPERTS * TASKS], F32)
+                nc.vector.tensor_copy(
+                    out=add_t[:],
+                    in_=add_np[:]
+                    .rearrange("q c n p -> q c (n p)")
+                    .unsqueeze(2)
+                    .to_broadcast([P, CHUNKS, BATCH, EXPERTS * TASKS]),
+                )
+                add_rows = psum.tile([ROWS, WIDTH], F32)
+                for c in range(CHUNKS):
+                    nc.tensor.transpose(
+                        add_rows[:, c * P : (c + 1) * P], add_t[:, c].rearrange("q b r -> q (b r)"), ident_f32[:]
+                    )
+                base = keep.tile([ROWS, WIDTH], F32)
+                nc.vector.tensor_tensor(out=base[:], in0=add_rows[:], in1=x_mix[:], op=ALU.add)
+
+                norm_rows = psum.tile([ROWS, 2, WIDTH], BF16)
+                for which, first_row in enumerate((ROW_GAIN, ROW_SHIFT)):
+                    norm_t = stage.tile([P, CHUNKS, BATCH, EXPERTS, TASKS], BF16)
+                    nc.vector.tensor_copy(
+                        out=norm_t[:],
+                        in_=small_t[:, :, first_row : first_row + EXPERTS]
+                        .unsqueeze(2)
+                        .unsqueeze(4)
+                        .to_broadcast([P, CHUNKS, BATCH, EXPERTS, TASKS]),
+                    )
+                    for c in range(CHUNKS):
+                        nc.tensor.transpose(
+                            norm_rows[:, which, c * P : (c + 1) * P],
+                            norm_t[:, c].rearrange("q b n p -> q (b n p)"),
+                            ident_bf[:],
+                        )
+
+        r = keep.tile([ROWS, WIDTH], F32)
+        nc.vector.tensor_tensor(out=r[:], in0=result[:], in1=base[:], op=ALU.add)
+        stats = keep.tile([ROWS, 6], F32)
+        nc.vector.bn_stats(out=stats[:], in_=r[:])
+        mean_var = keep.tile([ROWS, 2], F32)
+        nc.vector.bn_aggr(out=mean_var[:], in_=stats[:])
+        var_eps = keep.tile([ROWS, 1], F32)
+        nc.vector.tensor_scalar_add(out=var_eps[:], in0=mean_var[:, 1:2], scalar1=EPS)
+        rstd = keep.tile([ROWS, 1], F32)
+        nc.gpsimd.tensor_tensor(out=rstd[:], in0=var_eps[:], in1=minus_half[:], op=ALU.pow)
+        centred = keep.tile([ROWS, WIDTH], F32)
+        nc.vector.scalar_tensor_tensor(
+            out=centred[:], in0=r[:], scalar=mean_var[:, 0:1], in1=norm_rows[:, 0, :], op0=ALU.subtract, op1=ALU.mult
+        )
+        y = keep.tile([ROWS, WIDTH], F32)
+        nc.vector.scalar_tensor_tensor(
+            out=y[:], in0=centred[:], scalar=rstd[:], in1=norm_rows[:, 1, :], op0=ALU.mult, op1=ALU.add
+        )
+        nc.sync.dma_start(out=out.flatten_outer_dims(), in_=y[:])

@@ -15,18 +15,18 @@ BATCH = 4
 EXPERTS = 4
 TASKS = 8
 ROWS = BATCH * EXPERTS * TASKS
+ROWS_OF_B = EXPERTS * TASKS
 WIDTH = 512
-CHUNKS = WIDTH // P
+MATRICES = 2 * EXPERTS
 EPS = 1e-5
 
-ROW_TASK = 0
-ROW_B1 = ROW_TASK + TASKS
-ROW_B2 = ROW_B1 + EXPERTS
-ROW_GAIN = ROW_B2 + EXPERTS
-ROW_SHIFT = ROW_GAIN + EXPERTS
-SMALL_ROWS = ROW_SHIFT + EXPERTS
+HALF = WIDTH // 2
 
-VECTOR_COLS = 256
+VECTOR_COLS = 208
+
+QUANTISE_LAG = 1
+BIAS_LAG = 2
+SILU_LAG = 3
 
 FLOPS = 2 * 2 * ROWS * WIDTH * WIDTH
 
@@ -40,71 +40,81 @@ def regroup(engine_copy, grouped, raw, cols):
 
 def tile_hdmodel_pb_s_kernel(tc, xs_mix, task_emb, W1, b1, W2, b2, ln_g, ln_b, out):
     nc = tc.nc
+    halves = [slice(0, HALF), slice(HALF, WIDTH)]
     with (
         tc.tile_pool(name="keep", bufs=1) as keep,
-        tc.tile_pool(name="weights", bufs=2 * EXPERTS) as weights,
+        tc.tile_pool(name="weights", bufs=MATRICES) as weights,
         tc.tile_pool(name="stage", bufs=3) as stage,
         tc.psum_pool(name="psum", bufs=1) as psum,
-        tc.psum_pool(name="psum_hidden", bufs=2) as psum_hidden,
+        tc.psum_pool(name="psum_hidden", bufs=EXPERTS) as psum_hidden,
+        tc.manual_schedule(),
     ):
-        small = keep.tile([P, WIDTH], BF16)
-        nc.vector.memset(small[:], 0.0)
+        b1_rows = keep.tile([P, P], BF16)
+        nc.vector.memset(b1_rows[:], 0.0)
         h_grouped = keep.tile([P, EXPERTS, ROWS, PACK], BF16, align_bytes=64)
         nc.vector.memset(h_grouped[:], 0.0)
         minus_half = keep.tile([P, 1], F32)
         nc.vector.memset(minus_half[:], -0.5)
-        ident_bf = keep.tile([P, P], BF16)
-        make_identity(nc, ident_bf[:])
-        ident_f32 = keep.tile([P, P], F32)
-        make_identity(nc, ident_f32[:])
+        ident = keep.tile([P, P], BF16)
+        make_identity(nc, ident[:])
 
+        task_rows = keep.tile([ROWS, WIDTH], BF16)
+        nc.scalar.dma_start(
+            out=task_rows[:], in_=task_emb.unsqueeze(0).to_broadcast([BATCH * EXPERTS, TASKS, WIDTH])
+        )
+        nc.scalar.dma_start(
+            out=b1_rows[0 : EXPERTS * PACK, :], in_=b1.rearrange("n (t q) -> (n t) q", q=P)
+        )
         x_mix = keep.tile([ROWS, WIDTH], BF16)
         nc.sync.dma_start(out=x_mix[:], in_=xs_mix.flatten_outer_dims())
-        nc.scalar.dma_start(out=small[ROW_TASK : ROW_TASK + TASKS, :], in_=task_emb)
-        nc.scalar.dma_start(out=small[ROW_B1 : ROW_B1 + EXPERTS, :], in_=b1)
-        nc.scalar.dma_start(out=small[ROW_B2 : ROW_B2 + EXPERTS, :], in_=b2)
-        nc.scalar.dma_start(out=small[ROW_GAIN : ROW_GAIN + EXPERTS, :], in_=ln_g)
-        nc.scalar.dma_start(out=small[ROW_SHIFT : ROW_SHIFT + EXPERTS, :], in_=ln_b)
+
+        def load_expert_vector(rows_tile, vector):
+            for b in range(BATCH):
+                nc.sync.dma_start(
+                    out=rows_tile[b * ROWS_OF_B : (b + 1) * ROWS_OF_B, :],
+                    in_=vector.unsqueeze(1).to_broadcast([EXPERTS, TASKS, WIDTH]),
+                )
+
         raw_tiles = []
         for n in range(EXPERTS):
             raw = weights.tile([P, PACK, WIDTH], BF16)
             nc.sync.dma_start(out=raw[:], in_=W1[n].rearrange("(q j) w -> q j w", j=PACK))
             raw_tiles.append(raw)
+        b2_rows = keep.tile([ROWS, WIDTH], BF16)
+        load_expert_vector(b2_rows, b2)
         for n in range(EXPERTS):
             raw = weights.tile([P, PACK, WIDTH], BF16)
             nc.sync.dma_start(out=raw[:], in_=W2[n].rearrange("(t q) w -> q t w", q=P))
             raw_tiles.append(raw)
+        gain_rows = keep.tile([ROWS, WIDTH], BF16)
+        load_expert_vector(gain_rows, ln_g)
+        shift_rows = keep.tile([ROWS, WIDTH], BF16)
+        load_expert_vector(shift_rows, ln_b)
 
         warm = keep.tile([P, 1], F32)
         nc.scalar.activation(out=warm[:], in_=minus_half[:], func=ACT.Silu)
 
-        small_t_packed = psum.tile([P, PACK, P], BF16)
-        for j in range(PACK):
-            nc.tensor.transpose(
-                small_t_packed[:, j, :], small[:].rearrange("v (q j) -> v j q", j=PACK)[:, j, :], ident_bf[:]
-            )
-        task_t_packed = keep.tile([P, PACK, TASKS], BF16)
-        nc.vector.tensor_copy(out=task_t_packed[:], in_=small_t_packed[:, :, ROW_TASK : ROW_TASK + TASKS])
-        small_t_psum = psum.tile([P, CHUNKS, P], BF16)
-        for c in range(CHUNKS):
-            nc.tensor.transpose(small_t_psum[:, c, :], small[:, c * P : (c + 1) * P], ident_bf[:])
-        small_t = keep.tile([P, CHUNKS, SMALL_ROWS], BF16)
-        nc.vector.tensor_copy(out=small_t[:], in_=small_t_psum[:, :, 0:SMALL_ROWS])
-
+        x_bf = keep.tile([ROWS, PACK, P], BF16)
+        nc.vector.tensor_tensor(
+            out=x_bf[:],
+            in0=x_mix[:].rearrange("r (q j) -> r j q", j=PACK),
+            in1=task_rows[:].rearrange("r (q j) -> r j q", j=PACK),
+            op=ALU.add,
+        )
         x_t = psum.tile([P, PACK, ROWS], BF16)
         for j in range(PACK):
-            nc.tensor.transpose(
-                x_t[:, j, :], x_mix[:].rearrange("r (q j) -> r j q", j=PACK)[:, j, :], ident_bf[:]
-            )
+            nc.tensor.transpose(x_t[:, j, :], x_bf[:, j, :], ident[:])
+        b1_t_psum = psum.tile([P, P], BF16)
+        nc.tensor.transpose(b1_t_psum[:], b1_rows[:], ident[:])
+
+        base = keep.tile([ROWS, WIDTH], F32)
+        nc.vector.tensor_tensor(out=base[:], in0=x_mix[:], in1=task_rows[:], op=ALU.add)
+
         x_grouped = keep.tile([P, ROWS, PACK], BF16, align_bytes=64)
-        nc.vector.tensor_tensor(
-            out=x_grouped[:].rearrange("q (a p) j -> q a p j", p=TASKS),
-            in0=x_t[:].rearrange("q j (a p) -> q a p j", p=TASKS),
-            in1=task_t_packed[:]
-            .rearrange("q j p -> q p j")
-            .unsqueeze(1)
-            .to_broadcast([P, BATCH * EXPERTS, TASKS, PACK]),
-            op=ALU.add,
+        nc.vector.tensor_copy(out=x_grouped[:], in_=x_t[:].rearrange("q j r -> q r j"))
+        b1_t = keep.tile([P, EXPERTS, PACK], BF16)
+        nc.vector.tensor_copy(
+            out=b1_t[:], in_=b1_t_psum[:, 0 : EXPERTS * PACK].rearrange("q (n t) -> q n t", t=PACK)
         )
         x_codes = keep.tile([P, ROWS], U32, align_bytes=64)
         x_scales = keep.tile([P, ROWS], U8, align_bytes=64)
@@ -114,121 +124,126 @@ def tile_hdmodel_pb_s_kernel(tc, xs_mix, task_emb, W1, b1, W2, b2, ln_g, ln_b, o
             in_=x_grouped[:].rearrange("q r j -> q (r j)"),
         )
 
+        grouped_tiles = []
+        codes_tiles = []
+        scales_tiles = []
+        hidden_tiles = []
+        biased_tiles = []
         h_codes = keep.tile([P, EXPERTS, ROWS], U32, align_bytes=64)
         h_scales = keep.tile([P, EXPERTS, ROWS], U8, align_bytes=64)
-        result = psum.tile([ROWS, WIDTH], F32)
-        for layer in range(2):
-            for n in range(EXPERTS):
-                raw = raw_tiles[layer * EXPERTS + n]
-                grouped = stage.tile([P, WIDTH, PACK], BF16, align_bytes=64)
-                regroup(nc.vector.tensor_copy, grouped, raw, slice(0, VECTOR_COLS))
-                regroup(nc.scalar.copy, grouped, raw, slice(VECTOR_COLS, WIDTH))
-                w_codes = weights.tile([P, WIDTH], U32, align_bytes=64)
-                w_scales = weights.tile([P, WIDTH], U8, align_bytes=64)
-                nc.vector.quantize_mx(
-                    out=w_codes[:].bitcast(FP8X4),
-                    scales=w_scales[:],
-                    in_=grouped[:].rearrange("q w j -> q (w j)"),
-                )
-                if layer == 0:
-                    hidden = psum_hidden.tile([P, PACK, ROWS], F32)
-                    for t in range(PACK):
-                        nc.tensor.matmul_mx(
-                            out=hidden[:, t, :],
-                            lhsT=w_codes[:, t * P : (t + 1) * P].bitcast(FP8X4),
-                            lhsT_scale=w_scales[:, t * P : (t + 1) * P],
-                            rhs=x_codes[:].bitcast(FP8X4),
-                            rhs_scale=x_scales[:],
-                            start=True,
-                            stop=True,
-                        )
-                    biased = stage.tile([P, PACK, BATCH, TASKS], F32)
-                    nc.vector.tensor_tensor(
-                        out=biased[:],
-                        in0=hidden[:].rearrange("q t (b m p) -> q t b m p", b=BATCH, m=EXPERTS)[:, :, :, n, :],
-                        in1=small_t[:, :, ROW_B1 + n]
-                        .unsqueeze(2)
-                        .unsqueeze(3)
-                        .to_broadcast([P, PACK, BATCH, TASKS]),
-                        op=ALU.add,
-                    )
-                    nc.scalar.activation(
-                        out=h_grouped[:, n].rearrange("q (b m p) t -> q b m p t", b=BATCH, m=EXPERTS)[:, :, n, :, :],
-                        in_=biased[:].rearrange("q t b p -> q b p t"),
-                        func=ACT.Silu,
-                    )
-                    nc.vector.quantize_mx(
-                        out=h_codes[:, n, :].bitcast(FP8X4),
-                        scales=h_scales[:, n, :],
-                        in_=h_grouped[:, n].rearrange("q r t -> q (r t)"),
-                    )
-                else:
-                    nc.tensor.matmul_mx(
-                        out=result[:],
-                        lhsT=h_codes[:, n, :].bitcast(FP8X4),
-                        lhsT_scale=h_scales[:, n, :],
-                        rhs=w_codes[:].bitcast(FP8X4),
-                        rhs_scale=w_scales[:],
-                        start=(n == 0),
-                        stop=(n == EXPERTS - 1),
-                    )
-            if layer == 0:
-                add_np = keep.tile([P, CHUNKS, EXPERTS, TASKS], F32)
-                nc.vector.tensor_tensor(
-                    out=add_np[:],
-                    in0=small_t[:, :, ROW_B2 : ROW_B2 + EXPERTS].unsqueeze(3).to_broadcast([P, CHUNKS, EXPERTS, TASKS]),
-                    in1=small_t[:, :, ROW_TASK : ROW_TASK + TASKS].unsqueeze(2).to_broadcast([P, CHUNKS, EXPERTS, TASKS]),
-                    op=ALU.add,
-                )
-                add_t = keep.tile([P, CHUNKS, BATCH, EXPERTS * TASKS], F32)
-                nc.vector.tensor_copy(
-                    out=add_t[:],
-                    in_=add_np[:]
-                    .rearrange("q c n p -> q c (n p)")
-                    .unsqueeze(2)
-                    .to_broadcast([P, CHUNKS, BATCH, EXPERTS * TASKS]),
-                )
-                add_rows = psum.tile([ROWS, WIDTH], F32)
-                for c in range(CHUNKS):
-                    nc.tensor.transpose(
-                        add_rows[:, c * P : (c + 1) * P], add_t[:, c].rearrange("q b r -> q (b r)"), ident_f32[:]
-                    )
-                base = keep.tile([ROWS, WIDTH], F32)
-                nc.vector.tensor_tensor(out=base[:], in0=add_rows[:], in1=x_mix[:], op=ALU.add)
+        result = [psum.tile([ROWS, HALF], F32, name="result%d" % i) for i in range(len(halves))]
 
-                norm_rows = psum.tile([ROWS, 2, WIDTH], BF16)
-                for which, first_row in enumerate((ROW_GAIN, ROW_SHIFT)):
-                    norm_t = stage.tile([P, CHUNKS, BATCH, EXPERTS, TASKS], BF16)
-                    nc.vector.tensor_copy(
-                        out=norm_t[:],
-                        in_=small_t[:, :, first_row : first_row + EXPERTS]
-                        .unsqueeze(2)
-                        .unsqueeze(4)
-                        .to_broadcast([P, CHUNKS, BATCH, EXPERTS, TASKS]),
-                    )
-                    for c in range(CHUNKS):
-                        nc.tensor.transpose(
-                            norm_rows[:, which, c * P : (c + 1) * P],
-                            norm_t[:, c].rearrange("q b n p -> q (b n p)"),
-                            ident_bf[:],
-                        )
+        def regroup_matrix(m):
+            vector_cols = HALF if m == MATRICES - 1 else VECTOR_COLS
+            grouped = stage.tile([P, WIDTH, PACK], BF16, align_bytes=64)
+            regroup(nc.vector.tensor_copy, grouped, raw_tiles[m], slice(0, vector_cols))
+            regroup(nc.scalar.copy, grouped, raw_tiles[m], slice(vector_cols, WIDTH))
+            grouped_tiles.append(grouped)
+
+        def quantise_matrix(m):
+            w_codes = weights.tile([P, WIDTH], U32, align_bytes=64)
+            w_scales = weights.tile([P, WIDTH], U8, align_bytes=64)
+            for cols in halves:
+                nc.vector.quantize_mx(
+                    out=w_codes[:, cols].bitcast(FP8X4),
+                    scales=w_scales[:, cols],
+                    in_=grouped_tiles[m][:, cols, :].rearrange("q w j -> q (w j)"),
+                )
+            codes_tiles.append(w_codes)
+            scales_tiles.append(w_scales)
+
+        def first_product(n):
+            hidden = psum_hidden.tile([P, PACK, ROWS], F32)
+            for t in range(PACK):
+                nc.tensor.matmul_mx(
+                    out=hidden[:, t, :],
+                    lhsT=codes_tiles[n][:, t * P : (t + 1) * P].bitcast(FP8X4),
+                    lhsT_scale=scales_tiles[n][:, t * P : (t + 1) * P],
+                    rhs=x_codes[:].bitcast(FP8X4),
+                    rhs_scale=x_scales[:],
+                    start=True,
+                    stop=True,
+                )
+            hidden_tiles.append(hidden)
+
+        def add_bias(n):
+            biased = stage.tile([P, PACK, BATCH, TASKS], F32)
+            nc.vector.tensor_tensor(
+                out=biased[:],
+                in0=hidden_tiles[n][:].rearrange("q t (b e p) -> q t b e p", b=BATCH, e=EXPERTS)[:, :, :, n, :],
+                in1=b1_t[:, n, :].unsqueeze(2).unsqueeze(3).to_broadcast([P, PACK, BATCH, TASKS]),
+                op=ALU.add,
+            )
+            biased_tiles.append(biased)
+
+        def apply_silu(n):
+            nc.scalar.activation(
+                out=h_grouped[:, n].rearrange("q (b e p) t -> q b e p t", b=BATCH, e=EXPERTS)[:, :, n, :, :],
+                in_=biased_tiles[n][:].rearrange("q t b p -> q b p t"),
+                func=ACT.Silu,
+            )
+
+        def quantise_hidden(n):
+            nc.vector.quantize_mx(
+                out=h_codes[:, n, :].bitcast(FP8X4),
+                scales=h_scales[:, n, :],
+                in_=h_grouped[:, n].rearrange("q r t -> q (r t)"),
+            )
+
+        def second_product(n):
+            for i, cols in enumerate(halves):
+                nc.tensor.matmul_mx(
+                    out=result[i][:],
+                    lhsT=h_codes[:, n, :].bitcast(FP8X4),
+                    lhsT_scale=h_scales[:, n, :],
+                    rhs=codes_tiles[EXPERTS + n][:, cols].bitcast(FP8X4),
+                    rhs_scale=scales_tiles[EXPERTS + n][:, cols],
+                    start=(n == 0),
+                    stop=(n == EXPERTS - 1),
+                )
+
+        for step in range(MATRICES + QUANTISE_LAG):
+            if step - SILU_LAG in range(EXPERTS):
+                apply_silu(step - SILU_LAG)
+            if step in range(MATRICES):
+                regroup_matrix(step)
+            if step - QUANTISE_LAG in range(EXPERTS):
+                quantise_matrix(step - QUANTISE_LAG)
+                first_product(step - QUANTISE_LAG)
+            if step - QUANTISE_LAG in range(EXPERTS, MATRICES):
+                quantise_matrix(step - QUANTISE_LAG)
+                second_product(step - QUANTISE_LAG - EXPERTS)
+            if step - BIAS_LAG in range(EXPERTS):
+                add_bias(step - BIAS_LAG)
+            if step - SILU_LAG in range(EXPERTS):
+                quantise_hidden(step - SILU_LAG)
+            if step == BIAS_LAG + EXPERTS:
+                nc.vector.tensor_tensor(out=base[:], in0=base[:], in1=b2_rows[:], op=ALU.add)
 
         r = keep.tile([ROWS, WIDTH], F32)
-        nc.vector.tensor_tensor(out=r[:], in0=result[:], in1=base[:], op=ALU.add)
-        stats = keep.tile([ROWS, 6], F32)
-        nc.vector.bn_stats(out=stats[:], in_=r[:])
+        stats = keep.tile([ROWS, len(halves), 6], F32)
+        for i, cols in enumerate(halves):
+            nc.vector.tensor_tensor(out=r[:, cols], in0=result[i][:], in1=base[:, cols], op=ALU.add)
+            nc.vector.bn_stats(out=stats[:, i, :], in_=r[:, cols])
         mean_var = keep.tile([ROWS, 2], F32)
-        nc.vector.bn_aggr(out=mean_var[:], in_=stats[:])
+        nc.vector.bn_aggr(out=mean_var[:], in_=stats[:].rearrange("r i s -> r (i s)"))
         var_eps = keep.tile([ROWS, 1], F32)
         nc.vector.tensor_scalar_add(out=var_eps[:], in0=mean_var[:, 1:2], scalar1=EPS)
         rstd = keep.tile([ROWS, 1], F32)
         nc.gpsimd.tensor_tensor(out=rstd[:], in0=var_eps[:], in1=minus_half[:], op=ALU.pow)
         centred = keep.tile([ROWS, WIDTH], F32)
         nc.vector.scalar_tensor_tensor(
-            out=centred[:], in0=r[:], scalar=mean_var[:, 0:1], in1=norm_rows[:, 0, :], op0=ALU.subtract, op1=ALU.mult
+            out=centred[:], in0=r[:], scalar=mean_var[:, 0:1], in1=gain_rows[:], op0=ALU.subtract, op1=ALU.mult
         )
         y = keep.tile([ROWS, WIDTH], F32)
-        nc.vector.scalar_tensor_tensor(
-            out=y[:], in0=centred[:], scalar=rstd[:], in1=norm_rows[:, 1, :], op0=ALU.mult, op1=ALU.add
-        )
-        nc.sync.dma_start(out=out.flatten_outer_dims(), in_=y[:])
+        out_rows = out.flatten_outer_dims()
+        for cols in halves:
+            nc.vector.scalar_tensor_tensor(
+                out=y[:, cols],
+                in0=centred[:, cols],
+                scalar=rstd[:],
+                in1=shift_rows[:, cols],
+                op0=ALU.mult,
+                op1=ALU.add,
+            )
+            nc.sync.dma_start(out=out_rows[:, cols], in_=y[:, cols])

@@ -22,11 +22,11 @@ EPS = 1e-5
 
 HALF = WIDTH // 2
 
-VECTOR_COLS = 208
+VECTOR_COLS = 192
 
 QUANTISE_LAG = 1
 BIAS_LAG = 2
-SILU_LAG = 3
+SILU_LAG = 4
 
 FLOPS = 2 * 2 * ROWS * WIDTH * WIDTH
 
@@ -44,7 +44,7 @@ def tile_hdmodel_pb_s_kernel(tc, xs_mix, task_emb, W1, b1, W2, b2, ln_g, ln_b, o
     with (
         tc.tile_pool(name="keep", bufs=1) as keep,
         tc.tile_pool(name="weights", bufs=MATRICES) as weights,
-        tc.tile_pool(name="stage", bufs=3) as stage,
+        tc.tile_pool(name="experts", bufs=EXPERTS) as experts,
         tc.psum_pool(name="psum", bufs=1) as psum,
         tc.psum_pool(name="psum_hidden", bufs=EXPERTS) as psum_hidden,
         tc.manual_schedule(),
@@ -53,8 +53,10 @@ def tile_hdmodel_pb_s_kernel(tc, xs_mix, task_emb, W1, b1, W2, b2, ln_g, ln_b, o
         nc.vector.memset(b1_rows[:], 0.0)
         h_grouped = keep.tile([P, EXPERTS, ROWS, PACK], BF16, align_bytes=64)
         nc.vector.memset(h_grouped[:], 0.0)
-        minus_half = keep.tile([P, 1], F32)
-        nc.vector.memset(minus_half[:], -0.5)
+        one = keep.tile([P, 1], F32)
+        nc.vector.memset(one[:], 1.0)
+        eps = keep.tile([P, 1], F32)
+        nc.vector.memset(eps[:], EPS)
         ident = keep.tile([P, P], BF16)
         make_identity(nc, ident[:])
 
@@ -66,7 +68,6 @@ def tile_hdmodel_pb_s_kernel(tc, xs_mix, task_emb, W1, b1, W2, b2, ln_g, ln_b, o
             out=b1_rows[0 : EXPERTS * PACK, :], in_=b1.rearrange("n (t q) -> (n t) q", q=P)
         )
         x_mix = keep.tile([ROWS, WIDTH], BF16)
-        nc.sync.dma_start(out=x_mix[:], in_=xs_mix.flatten_outer_dims())
 
         def load_expert_vector(rows_tile, vector):
             for b in range(BATCH):
@@ -78,7 +79,13 @@ def tile_hdmodel_pb_s_kernel(tc, xs_mix, task_emb, W1, b1, W2, b2, ln_g, ln_b, o
         raw_tiles = []
         for n in range(EXPERTS):
             raw = weights.tile([P, PACK, WIDTH], BF16)
-            nc.sync.dma_start(out=raw[:], in_=W1[n].rearrange("(q j) w -> q j w", j=PACK))
+            w1_rows = W1[n].rearrange("(q j) w -> q j w", j=PACK)
+            if n == 0:
+                nc.sync.dma_start(out=raw[:, :, VECTOR_COLS:WIDTH], in_=w1_rows[:, :, VECTOR_COLS:WIDTH])
+                nc.sync.dma_start(out=x_mix[:], in_=xs_mix.flatten_outer_dims())
+                nc.sync.dma_start(out=raw[:, :, 0:VECTOR_COLS], in_=w1_rows[:, :, 0:VECTOR_COLS])
+            else:
+                nc.sync.dma_start(out=raw[:], in_=w1_rows)
             raw_tiles.append(raw)
         b2_rows = keep.tile([ROWS, WIDTH], BF16)
         load_expert_vector(b2_rows, b2)
@@ -91,8 +98,8 @@ def tile_hdmodel_pb_s_kernel(tc, xs_mix, task_emb, W1, b1, W2, b2, ln_g, ln_b, o
         shift_rows = keep.tile([ROWS, WIDTH], BF16)
         load_expert_vector(shift_rows, ln_b)
 
-        warm = keep.tile([P, 1], F32)
-        nc.scalar.activation(out=warm[:], in_=minus_half[:], func=ACT.Silu)
+        warm_silu = keep.tile([P, 1], F32)
+        nc.scalar.activation(out=warm_silu[:], in_=one[:], func=ACT.Silu)
 
         x_bf = keep.tile([ROWS, PACK, P], BF16)
         nc.vector.tensor_tensor(
@@ -111,18 +118,9 @@ def tile_hdmodel_pb_s_kernel(tc, xs_mix, task_emb, W1, b1, W2, b2, ln_g, ln_b, o
         nc.vector.tensor_tensor(out=base[:], in0=x_mix[:], in1=task_rows[:], op=ALU.add)
 
         x_grouped = keep.tile([P, ROWS, PACK], BF16, align_bytes=64)
-        nc.vector.tensor_copy(out=x_grouped[:], in_=x_t[:].rearrange("q j r -> q r j"))
         b1_t = keep.tile([P, EXPERTS, PACK], BF16)
-        nc.vector.tensor_copy(
-            out=b1_t[:], in_=b1_t_psum[:, 0 : EXPERTS * PACK].rearrange("q (n t) -> q n t", t=PACK)
-        )
         x_codes = keep.tile([P, ROWS], U32, align_bytes=64)
         x_scales = keep.tile([P, ROWS], U8, align_bytes=64)
-        nc.vector.quantize_mx(
-            out=x_codes[:].bitcast(FP8X4),
-            scales=x_scales[:],
-            in_=x_grouped[:].rearrange("q r j -> q (r j)"),
-        )
 
         grouped_tiles = []
         codes_tiles = []
@@ -133,9 +131,20 @@ def tile_hdmodel_pb_s_kernel(tc, xs_mix, task_emb, W1, b1, W2, b2, ln_g, ln_b, o
         h_scales = keep.tile([P, EXPERTS, ROWS], U8, align_bytes=64)
         result = [psum.tile([ROWS, HALF], F32, name="result%d" % i) for i in range(len(halves))]
 
+        def quantise_rows():
+            nc.vector.tensor_copy(out=x_grouped[:], in_=x_t[:].rearrange("q j r -> q r j"))
+            nc.vector.tensor_copy(
+                out=b1_t[:], in_=b1_t_psum[:, 0 : EXPERTS * PACK].rearrange("q (n t) -> q n t", t=PACK)
+            )
+            nc.vector.quantize_mx(
+                out=x_codes[:].bitcast(FP8X4),
+                scales=x_scales[:],
+                in_=x_grouped[:].rearrange("q r j -> q (r j)"),
+            )
+
         def regroup_matrix(m):
             vector_cols = HALF if m == MATRICES - 1 else VECTOR_COLS
-            grouped = stage.tile([P, WIDTH, PACK], BF16, align_bytes=64)
+            grouped = weights.tile([P, WIDTH, PACK], BF16, align_bytes=64)
             regroup(nc.vector.tensor_copy, grouped, raw_tiles[m], slice(0, vector_cols))
             regroup(nc.scalar.copy, grouped, raw_tiles[m], slice(vector_cols, WIDTH))
             grouped_tiles.append(grouped)
@@ -167,7 +176,7 @@ def tile_hdmodel_pb_s_kernel(tc, xs_mix, task_emb, W1, b1, W2, b2, ln_g, ln_b, o
             hidden_tiles.append(hidden)
 
         def add_bias(n):
-            biased = stage.tile([P, PACK, BATCH, TASKS], F32)
+            biased = experts.tile([P, PACK, BATCH, TASKS], F32)
             nc.vector.tensor_tensor(
                 out=biased[:],
                 in0=hidden_tiles[n][:].rearrange("q t (b e p) -> q t b e p", b=BATCH, e=EXPERTS)[:, :, :, n, :],
@@ -207,6 +216,8 @@ def tile_hdmodel_pb_s_kernel(tc, xs_mix, task_emb, W1, b1, W2, b2, ln_g, ln_b, o
                 apply_silu(step - SILU_LAG)
             if step in range(MATRICES):
                 regroup_matrix(step)
+            if step == QUANTISE_LAG:
+                quantise_rows()
             if step - QUANTISE_LAG in range(EXPERTS):
                 quantise_matrix(step - QUANTISE_LAG)
                 first_product(step - QUANTISE_LAG)
@@ -220,6 +231,9 @@ def tile_hdmodel_pb_s_kernel(tc, xs_mix, task_emb, W1, b1, W2, b2, ln_g, ln_b, o
             if step == BIAS_LAG + EXPERTS:
                 nc.vector.tensor_tensor(out=base[:], in0=base[:], in1=b2_rows[:], op=ALU.add)
 
+        warm_sqrt = keep.tile([P, 1], F32)
+        nc.scalar.activation(out=warm_sqrt[:], in_=one[:], func=ACT.Sqrt)
+
         r = keep.tile([ROWS, WIDTH], F32)
         stats = keep.tile([ROWS, len(halves), 6], F32)
         for i, cols in enumerate(halves):
@@ -227,14 +241,14 @@ def tile_hdmodel_pb_s_kernel(tc, xs_mix, task_emb, W1, b1, W2, b2, ln_g, ln_b, o
             nc.vector.bn_stats(out=stats[:, i, :], in_=r[:, cols])
         mean_var = keep.tile([ROWS, 2], F32)
         nc.vector.bn_aggr(out=mean_var[:], in_=stats[:].rearrange("r i s -> r (i s)"))
-        var_eps = keep.tile([ROWS, 1], F32)
-        nc.vector.tensor_scalar_add(out=var_eps[:], in0=mean_var[:, 1:2], scalar1=EPS)
-        rstd = keep.tile([ROWS, 1], F32)
-        nc.gpsimd.tensor_tensor(out=rstd[:], in0=var_eps[:], in1=minus_half[:], op=ALU.pow)
+        std = keep.tile([ROWS, 1], F32)
+        nc.scalar.activation(out=std[:], in_=mean_var[:, 1:2], func=ACT.Sqrt, bias=eps[:])
         centred = keep.tile([ROWS, WIDTH], F32)
         nc.vector.scalar_tensor_tensor(
             out=centred[:], in0=r[:], scalar=mean_var[:, 0:1], in1=gain_rows[:], op0=ALU.subtract, op1=ALU.mult
         )
+        rstd = keep.tile([ROWS, 1], F32)
+        nc.vector.reciprocal(out=rstd[:], in_=std[:])
         y = keep.tile([ROWS, WIDTH], F32)
         out_rows = out.flatten_outer_dims()
         for cols in halves:

@@ -17,10 +17,15 @@ TASKS = 8
 ROWS = BATCH * EXPERTS * TASKS
 ROWS_OF_B = EXPERTS * TASKS
 WIDTH = 512
+CHUNKS = WIDTH // P
+HALF = WIDTH // 2
 MATRICES = 2 * EXPERTS
 EPS = 1e-5
 
-HALF = WIDTH // 2
+ROW_TASK = 0
+ROW_B1 = ROW_TASK + TASKS
+ROW_B2 = ROW_B1 + EXPERTS
+SMALL_ROWS = ROW_B2 + EXPERTS
 
 VECTOR_COLS = 192
 
@@ -46,101 +51,75 @@ def tile_hdmodel_pb_s_kernel(tc, xs_mix, task_emb, W1, b1, W2, b2, ln_g, ln_b, o
         tc.tile_pool(name="weights", bufs=MATRICES) as weights,
         tc.tile_pool(name="experts", bufs=EXPERTS) as experts,
         tc.psum_pool(name="psum", bufs=1) as psum,
-        tc.psum_pool(name="psum_hidden", bufs=EXPERTS) as psum_hidden,
+        tc.psum_pool(name="psum_hidden", bufs=2) as psum_hidden,
         tc.manual_schedule(),
     ):
-        b1_rows = keep.tile([P, P], BF16)
-        nc.vector.memset(b1_rows[:], 0.0)
-        h_grouped = keep.tile([P, EXPERTS, ROWS, PACK], BF16, align_bytes=64)
-        nc.vector.memset(h_grouped[:], 0.0)
+        small = keep.tile([P, WIDTH], BF16)
+        nc.gpsimd.memset(small[:], 0.0)
+        ident = keep.tile([P, P], BF16)
+        make_identity(nc, ident[:])
+        ident_f32 = keep.tile([P, P], F32)
+        make_identity(nc, ident_f32[:])
         one = keep.tile([P, 1], F32)
         nc.vector.memset(one[:], 1.0)
         eps = keep.tile([P, 1], F32)
         nc.vector.memset(eps[:], EPS)
-        ident = keep.tile([P, P], BF16)
-        make_identity(nc, ident[:])
+        h_grouped = keep.tile([P, EXPERTS, ROWS, PACK], BF16, align_bytes=64)
+        nc.vector.memset(h_grouped[:], 0.0)
 
-        task_rows = keep.tile([ROWS, WIDTH], BF16)
-        nc.scalar.dma_start(
-            out=task_rows[:], in_=task_emb.unsqueeze(0).to_broadcast([BATCH * EXPERTS, TASKS, WIDTH])
-        )
-        nc.scalar.dma_start(
-            out=b1_rows[0 : EXPERTS * PACK, :], in_=b1.rearrange("n (t q) -> (n t) q", q=P)
-        )
         x_mix = keep.tile([ROWS, WIDTH], BF16)
-
-        def load_expert_vector(rows_tile, vector):
+        raw_tiles = []
+        for n in range(EXPERTS):
+            raw = weights.tile([P, PACK, WIDTH], BF16)
+            nc.sync.dma_start(out=raw[:], in_=W1[n].rearrange("(q j) w -> q j w", j=PACK))
+            raw_tiles.append(raw)
+            if n == 0:
+                nc.sync.dma_start(out=small[ROW_TASK : ROW_TASK + TASKS, :], in_=task_emb)
+                nc.sync.dma_start(out=small[ROW_B1 : ROW_B1 + EXPERTS, :], in_=b1)
+                nc.sync.dma_start(out=small[ROW_B2 : ROW_B2 + EXPERTS, :], in_=b2)
+                nc.sync.dma_start(out=x_mix[:], in_=xs_mix.flatten_outer_dims())
+        for n in range(EXPERTS):
+            raw = weights.tile([P, PACK, WIDTH], BF16)
+            nc.sync.dma_start(out=raw[:], in_=W2[n].rearrange("(t q) w -> q t w", q=P))
+            raw_tiles.append(raw)
+        norm_rows = []
+        for vector in (ln_g, ln_b):
+            rows_tile = keep.tile([ROWS, WIDTH], BF16, name="norm_rows%d" % len(norm_rows))
             for b in range(BATCH):
                 nc.sync.dma_start(
                     out=rows_tile[b * ROWS_OF_B : (b + 1) * ROWS_OF_B, :],
                     in_=vector.unsqueeze(1).to_broadcast([EXPERTS, TASKS, WIDTH]),
                 )
-
-        raw_tiles = []
-        for n in range(EXPERTS):
-            raw = weights.tile([P, PACK, WIDTH], BF16)
-            w1_rows = W1[n].rearrange("(q j) w -> q j w", j=PACK)
-            if n == 0:
-                nc.sync.dma_start(out=raw[:, :, VECTOR_COLS:WIDTH], in_=w1_rows[:, :, VECTOR_COLS:WIDTH])
-                nc.sync.dma_start(out=x_mix[:], in_=xs_mix.flatten_outer_dims())
-                nc.sync.dma_start(out=raw[:, :, 0:VECTOR_COLS], in_=w1_rows[:, :, 0:VECTOR_COLS])
-            else:
-                nc.sync.dma_start(out=raw[:], in_=w1_rows)
-            raw_tiles.append(raw)
-        b2_rows = keep.tile([ROWS, WIDTH], BF16)
-        load_expert_vector(b2_rows, b2)
-        for n in range(EXPERTS):
-            raw = weights.tile([P, PACK, WIDTH], BF16)
-            nc.sync.dma_start(out=raw[:], in_=W2[n].rearrange("(t q) w -> q t w", q=P))
-            raw_tiles.append(raw)
-        gain_rows = keep.tile([ROWS, WIDTH], BF16)
-        load_expert_vector(gain_rows, ln_g)
-        shift_rows = keep.tile([ROWS, WIDTH], BF16)
-        load_expert_vector(shift_rows, ln_b)
+            norm_rows.append(rows_tile)
+        gain_rows, shift_rows = norm_rows
 
         warm_silu = keep.tile([P, 1], F32)
         nc.scalar.activation(out=warm_silu[:], in_=one[:], func=ACT.Silu)
 
-        x_bf = keep.tile([ROWS, PACK, P], BF16)
-        nc.vector.tensor_tensor(
-            out=x_bf[:],
-            in0=x_mix[:].rearrange("r (q j) -> r j q", j=PACK),
-            in1=task_rows[:].rearrange("r (q j) -> r j q", j=PACK),
-            op=ALU.add,
-        )
         x_t = psum.tile([P, PACK, ROWS], BF16)
-        for j in range(PACK):
-            nc.tensor.transpose(x_t[:, j, :], x_bf[:, j, :], ident[:])
-        b1_t_psum = psum.tile([P, P], BF16)
-        nc.tensor.transpose(b1_t_psum[:], b1_rows[:], ident[:])
-
-        base = keep.tile([ROWS, WIDTH], F32)
-        nc.vector.tensor_tensor(out=base[:], in0=x_mix[:], in1=task_rows[:], op=ALU.add)
-
-        x_grouped = keep.tile([P, ROWS, PACK], BF16, align_bytes=64)
-        b1_t = keep.tile([P, EXPERTS, PACK], BF16)
-        x_codes = keep.tile([P, ROWS], U32, align_bytes=64)
-        x_scales = keep.tile([P, ROWS], U8, align_bytes=64)
+        small_t_packed = psum.tile([P, PACK, P], BF16)
+        for source, target in ((small, small_t_packed), (x_mix, x_t)):
+            for j in range(PACK):
+                nc.tensor.transpose(
+                    target[:, j, :], source[:].rearrange("r (q j) -> r j q", j=PACK)[:, j, :], ident[:]
+                )
+        small_t_psum = psum.tile([P, CHUNKS, P], BF16)
+        for c in range(CHUNKS):
+            nc.tensor.transpose(small_t_psum[:, c, :], small[:, c * P : (c + 1) * P], ident[:])
 
         grouped_tiles = []
         codes_tiles = []
         scales_tiles = []
         hidden_tiles = []
         biased_tiles = []
+        small_t = keep.tile([P, CHUNKS, SMALL_ROWS], BF16)
+        x_codes = keep.tile([P, ROWS], U32, align_bytes=64)
+        x_scales = keep.tile([P, ROWS], U8, align_bytes=64)
         h_codes = keep.tile([P, EXPERTS, ROWS], U32, align_bytes=64)
         h_scales = keep.tile([P, EXPERTS, ROWS], U8, align_bytes=64)
+        add_rows = psum.tile([ROWS, WIDTH], F32)
+        base = keep.tile([ROWS, WIDTH], F32)
         result = [psum.tile([ROWS, HALF], F32, name="result%d" % i) for i in range(len(halves))]
-
-        def quantise_rows():
-            nc.vector.tensor_copy(out=x_grouped[:], in_=x_t[:].rearrange("q j r -> q r j"))
-            nc.vector.tensor_copy(
-                out=b1_t[:], in_=b1_t_psum[:, 0 : EXPERTS * PACK].rearrange("q (n t) -> q n t", t=PACK)
-            )
-            nc.vector.quantize_mx(
-                out=x_codes[:].bitcast(FP8X4),
-                scales=x_scales[:],
-                in_=x_grouped[:].rearrange("q r j -> q (r j)"),
-            )
 
         def regroup_matrix(m):
             vector_cols = HALF if m == MATRICES - 1 else VECTOR_COLS
@@ -161,6 +140,47 @@ def tile_hdmodel_pb_s_kernel(tc, xs_mix, task_emb, W1, b1, W2, b2, ln_g, ln_b, o
             codes_tiles.append(w_codes)
             scales_tiles.append(w_scales)
 
+        def quantise_rows():
+            task_t_packed = keep.tile([P, PACK, TASKS], BF16)
+            nc.vector.tensor_copy(out=task_t_packed[:], in_=small_t_packed[:, :, ROW_TASK : ROW_TASK + TASKS])
+            x_grouped = keep.tile([P, ROWS, PACK], BF16, align_bytes=64)
+            nc.vector.tensor_tensor(
+                out=x_grouped[:].rearrange("q (a p) j -> q a p j", p=TASKS),
+                in0=x_t[:].rearrange("q j (a p) -> q a p j", p=TASKS),
+                in1=task_t_packed[:]
+                .rearrange("q j p -> q p j")
+                .unsqueeze(1)
+                .to_broadcast([P, BATCH * EXPERTS, TASKS, PACK]),
+                op=ALU.add,
+            )
+            nc.vector.tensor_copy(out=small_t[:], in_=small_t_psum[:, :, 0:SMALL_ROWS])
+            nc.vector.quantize_mx(
+                out=x_codes[:].bitcast(FP8X4),
+                scales=x_scales[:],
+                in_=x_grouped[:].rearrange("q r j -> q (r j)"),
+            )
+
+        def spread_residual_vectors():
+            add_np = keep.tile([P, CHUNKS, EXPERTS, TASKS], F32)
+            nc.vector.tensor_tensor(
+                out=add_np[:],
+                in0=small_t[:, :, ROW_B2 : ROW_B2 + EXPERTS].unsqueeze(3).to_broadcast([P, CHUNKS, EXPERTS, TASKS]),
+                in1=small_t[:, :, ROW_TASK : ROW_TASK + TASKS].unsqueeze(2).to_broadcast([P, CHUNKS, EXPERTS, TASKS]),
+                op=ALU.add,
+            )
+            add_t = keep.tile([P, CHUNKS, BATCH, ROWS_OF_B], F32)
+            nc.vector.tensor_copy(
+                out=add_t[:],
+                in_=add_np[:]
+                .rearrange("q c n p -> q c (n p)")
+                .unsqueeze(2)
+                .to_broadcast([P, CHUNKS, BATCH, ROWS_OF_B]),
+            )
+            for c in range(CHUNKS):
+                nc.tensor.transpose(
+                    add_rows[:, c * P : (c + 1) * P], add_t[:, c].rearrange("q b r -> q (b r)"), ident_f32[:]
+                )
+
         def first_product(n):
             hidden = psum_hidden.tile([P, PACK, ROWS], F32)
             for t in range(PACK):
@@ -180,7 +200,7 @@ def tile_hdmodel_pb_s_kernel(tc, xs_mix, task_emb, W1, b1, W2, b2, ln_g, ln_b, o
             nc.vector.tensor_tensor(
                 out=biased[:],
                 in0=hidden_tiles[n][:].rearrange("q t (b e p) -> q t b e p", b=BATCH, e=EXPERTS)[:, :, :, n, :],
-                in1=b1_t[:, n, :].unsqueeze(2).unsqueeze(3).to_broadcast([P, PACK, BATCH, TASKS]),
+                in1=small_t[:, :, ROW_B1 + n].unsqueeze(2).unsqueeze(3).to_broadcast([P, PACK, BATCH, TASKS]),
                 op=ALU.add,
             )
             biased_tiles.append(biased)
@@ -229,7 +249,9 @@ def tile_hdmodel_pb_s_kernel(tc, xs_mix, task_emb, W1, b1, W2, b2, ln_g, ln_b, o
             if step - SILU_LAG in range(EXPERTS):
                 quantise_hidden(step - SILU_LAG)
             if step == BIAS_LAG + EXPERTS:
-                nc.vector.tensor_tensor(out=base[:], in0=base[:], in1=b2_rows[:], op=ALU.add)
+                spread_residual_vectors()
+            if step == BIAS_LAG + EXPERTS + 1:
+                nc.vector.tensor_tensor(out=base[:], in0=add_rows[:], in1=x_mix[:], op=ALU.add)
 
         warm_sqrt = keep.tile([P, 1], F32)
         nc.scalar.activation(out=warm_sqrt[:], in_=one[:], func=ACT.Sqrt)
@@ -238,6 +260,7 @@ def tile_hdmodel_pb_s_kernel(tc, xs_mix, task_emb, W1, b1, W2, b2, ln_g, ln_b, o
         stats = keep.tile([ROWS, len(halves), 6], F32)
         for i, cols in enumerate(halves):
             nc.vector.tensor_tensor(out=r[:, cols], in0=result[i][:], in1=base[:, cols], op=ALU.add)
+        for i, cols in enumerate(halves):
             nc.vector.bn_stats(out=stats[:, i, :], in_=r[:, cols])
         mean_var = keep.tile([ROWS, 2], F32)
         nc.vector.bn_aggr(out=mean_var[:], in_=stats[:].rearrange("r i s -> r (i s)"))

@@ -28,6 +28,7 @@ ROW_B2 = ROW_B1 + EXPERTS
 SMALL_ROWS = ROW_B2 + EXPERTS
 
 VECTOR_COLS = 192
+LAST_VECTOR_COLS = 64
 
 QUANTISE_LAG = 1
 BIAS_LAG = 2
@@ -122,16 +123,18 @@ def tile_hdmodel_pb_s_kernel(tc, xs_mix, task_emb, W1, b1, W2, b2, ln_g, ln_b, o
         result = [psum.tile([ROWS, HALF], F32, name="result%d" % i) for i in range(len(halves))]
 
         def regroup_matrix(m):
-            vector_cols = HALF if m == MATRICES - 1 else VECTOR_COLS
+            last = m == MATRICES - 1
+            vector_cols = LAST_VECTOR_COLS if last else VECTOR_COLS
             grouped = weights.tile([P, WIDTH, PACK], BF16, align_bytes=64)
             regroup(nc.vector.tensor_copy, grouped, raw_tiles[m], slice(0, vector_cols))
-            regroup(nc.scalar.copy, grouped, raw_tiles[m], slice(vector_cols, WIDTH))
+            for cols in [slice(vector_cols, HALF), halves[1]] if last else [slice(vector_cols, WIDTH)]:
+                regroup(nc.scalar.copy, grouped, raw_tiles[m], cols)
             grouped_tiles.append(grouped)
 
         def quantise_matrix(m):
             w_codes = weights.tile([P, WIDTH], U32, align_bytes=64)
             w_scales = weights.tile([P, WIDTH], U8, align_bytes=64)
-            for cols in halves:
+            for cols in halves if m == MATRICES - 1 else [slice(0, WIDTH)]:
                 nc.vector.quantize_mx(
                     out=w_codes[:, cols].bitcast(FP8X4),
                     scales=w_scales[:, cols],
@@ -236,7 +239,7 @@ def tile_hdmodel_pb_s_kernel(tc, xs_mix, task_emb, W1, b1, W2, b2, ln_g, ln_b, o
                 apply_silu(step - SILU_LAG)
             if step in range(MATRICES):
                 regroup_matrix(step)
-            if step == QUANTISE_LAG:
+            if step == 0:
                 quantise_rows()
             if step - QUANTISE_LAG in range(EXPERTS):
                 quantise_matrix(step - QUANTISE_LAG)
@@ -248,9 +251,9 @@ def tile_hdmodel_pb_s_kernel(tc, xs_mix, task_emb, W1, b1, W2, b2, ln_g, ln_b, o
                 add_bias(step - BIAS_LAG)
             if step - SILU_LAG in range(EXPERTS):
                 quantise_hidden(step - SILU_LAG)
-            if step == BIAS_LAG + EXPERTS:
+            if step == QUANTISE_LAG:
                 spread_residual_vectors()
-            if step == BIAS_LAG + EXPERTS + 1:
+            if step == BIAS_LAG + EXPERTS:
                 nc.vector.tensor_tensor(out=base[:], in0=add_rows[:], in1=x_mix[:], op=ALU.add)
 
         warm_sqrt = keep.tile([P, 1], F32)

@@ -27,7 +27,8 @@ ROW_B1 = ROW_TASK + TASKS
 ROW_B2 = ROW_B1 + EXPERTS
 SMALL_ROWS = ROW_B2 + EXPERTS
 
-VECTOR_COLS = 192
+VECTOR_COLS = 208
+FIRST_VECTOR_COLS = 128
 LAST_VECTOR_COLS = 64
 
 QUANTISE_LAG = 1
@@ -56,7 +57,7 @@ def tile_hdmodel_pb_s_kernel(tc, xs_mix, task_emb, W1, b1, W2, b2, ln_g, ln_b, o
         tc.manual_schedule(),
     ):
         small = keep.tile([P, WIDTH], BF16)
-        nc.gpsimd.memset(small[:], 0.0)
+        nc.vector.memset(small[:].bitcast(F32), 0.0)
         ident = keep.tile([P, P], BF16)
         make_identity(nc, ident[:])
         ident_f32 = keep.tile([P, P], F32)
@@ -66,19 +67,20 @@ def tile_hdmodel_pb_s_kernel(tc, xs_mix, task_emb, W1, b1, W2, b2, ln_g, ln_b, o
         eps = keep.tile([P, 1], F32)
         nc.vector.memset(eps[:], EPS)
         h_grouped = keep.tile([P, EXPERTS, ROWS, PACK], BF16, align_bytes=64)
-        nc.vector.memset(h_grouped[:], 0.0)
+        nc.vector.memset(h_grouped[:].rearrange("q n r t -> q (n r t)").bitcast(F32), 0.0)
 
         x_mix = keep.tile([ROWS, WIDTH], BF16)
+        nc.sync.dma_start(out=x_mix[:], in_=xs_mix.flatten_outer_dims())
         raw_tiles = []
         for n in range(EXPERTS):
             raw = weights.tile([P, PACK, WIDTH], BF16)
-            nc.sync.dma_start(out=raw[:], in_=W1[n].rearrange("(q j) w -> q j w", j=PACK))
+            for cols in halves if n == 0 else [slice(0, WIDTH)]:
+                nc.sync.dma_start(out=raw[:, :, cols], in_=W1[n].rearrange("(q j) w -> q j w", j=PACK)[:, :, cols])
+                if cols == halves[0]:
+                    nc.sync.dma_start(out=small[ROW_TASK : ROW_TASK + TASKS, :], in_=task_emb)
+                    nc.sync.dma_start(out=small[ROW_B1 : ROW_B1 + EXPERTS, :], in_=b1)
+                    nc.sync.dma_start(out=small[ROW_B2 : ROW_B2 + EXPERTS, :], in_=b2)
             raw_tiles.append(raw)
-            if n == 0:
-                nc.sync.dma_start(out=small[ROW_TASK : ROW_TASK + TASKS, :], in_=task_emb)
-                nc.sync.dma_start(out=small[ROW_B1 : ROW_B1 + EXPERTS, :], in_=b1)
-                nc.sync.dma_start(out=small[ROW_B2 : ROW_B2 + EXPERTS, :], in_=b2)
-                nc.sync.dma_start(out=x_mix[:], in_=xs_mix.flatten_outer_dims())
         for n in range(EXPERTS):
             raw = weights.tile([P, PACK, WIDTH], BF16)
             nc.sync.dma_start(out=raw[:], in_=W2[n].rearrange("(t q) w -> q t w", q=P))
@@ -99,7 +101,7 @@ def tile_hdmodel_pb_s_kernel(tc, xs_mix, task_emb, W1, b1, W2, b2, ln_g, ln_b, o
 
         x_t = psum.tile([P, PACK, ROWS], BF16)
         small_t_packed = psum.tile([P, PACK, P], BF16)
-        for source, target in ((small, small_t_packed), (x_mix, x_t)):
+        for source, target in ((x_mix, x_t), (small, small_t_packed)):
             for j in range(PACK):
                 nc.tensor.transpose(
                     target[:, j, :], source[:].rearrange("r (q j) -> r j q", j=PACK)[:, j, :], ident[:]
@@ -118,14 +120,22 @@ def tile_hdmodel_pb_s_kernel(tc, xs_mix, task_emb, W1, b1, W2, b2, ln_g, ln_b, o
         x_scales = keep.tile([P, ROWS], U8, align_bytes=64)
         h_codes = keep.tile([P, EXPERTS, ROWS], U32, align_bytes=64)
         h_scales = keep.tile([P, EXPERTS, ROWS], U8, align_bytes=64)
+        add_np = keep.tile([P, CHUNKS, EXPERTS, TASKS], F32)
         add_rows = psum.tile([ROWS, WIDTH], F32)
         base = keep.tile([ROWS, WIDTH], F32)
         result = [psum.tile([ROWS, HALF], F32, name="result%d" % i) for i in range(len(halves))]
 
         def regroup_matrix(m):
+            grouped = weights.tile([P, WIDTH, PACK], BF16, align_bytes=64)
+            if m == 0:
+                scalar_cols = WIDTH - FIRST_VECTOR_COLS
+                for cols in (halves[0], slice(HALF, scalar_cols)):
+                    regroup(nc.scalar.copy, grouped, raw_tiles[m], cols)
+                regroup(nc.vector.tensor_copy, grouped, raw_tiles[m], slice(scalar_cols, WIDTH))
+                grouped_tiles.append(grouped)
+                return
             last = m == MATRICES - 1
             vector_cols = LAST_VECTOR_COLS if last else VECTOR_COLS
-            grouped = weights.tile([P, WIDTH, PACK], BF16, align_bytes=64)
             regroup(nc.vector.tensor_copy, grouped, raw_tiles[m], slice(0, vector_cols))
             for cols in [slice(vector_cols, HALF), halves[1]] if last else [slice(vector_cols, WIDTH)]:
                 regroup(nc.scalar.copy, grouped, raw_tiles[m], cols)
@@ -157,6 +167,12 @@ def tile_hdmodel_pb_s_kernel(tc, xs_mix, task_emb, W1, b1, W2, b2, ln_g, ln_b, o
                 op=ALU.add,
             )
             nc.vector.tensor_copy(out=small_t[:], in_=small_t_psum[:, :, 0:SMALL_ROWS])
+            nc.vector.tensor_tensor(
+                out=add_np[:],
+                in0=small_t[:, :, ROW_B2 : ROW_B2 + EXPERTS].unsqueeze(3).to_broadcast([P, CHUNKS, EXPERTS, TASKS]),
+                in1=small_t[:, :, ROW_TASK : ROW_TASK + TASKS].unsqueeze(2).to_broadcast([P, CHUNKS, EXPERTS, TASKS]),
+                op=ALU.add,
+            )
             nc.vector.quantize_mx(
                 out=x_codes[:].bitcast(FP8X4),
                 scales=x_scales[:],
@@ -164,13 +180,6 @@ def tile_hdmodel_pb_s_kernel(tc, xs_mix, task_emb, W1, b1, W2, b2, ln_g, ln_b, o
             )
 
         def spread_residual_vectors():
-            add_np = keep.tile([P, CHUNKS, EXPERTS, TASKS], F32)
-            nc.vector.tensor_tensor(
-                out=add_np[:],
-                in0=small_t[:, :, ROW_B2 : ROW_B2 + EXPERTS].unsqueeze(3).to_broadcast([P, CHUNKS, EXPERTS, TASKS]),
-                in1=small_t[:, :, ROW_TASK : ROW_TASK + TASKS].unsqueeze(2).to_broadcast([P, CHUNKS, EXPERTS, TASKS]),
-                op=ALU.add,
-            )
             add_t = keep.tile([P, CHUNKS, BATCH, ROWS_OF_B], F32)
             nc.vector.tensor_copy(
                 out=add_t[:],
@@ -241,6 +250,7 @@ def tile_hdmodel_pb_s_kernel(tc, xs_mix, task_emb, W1, b1, W2, b2, ln_g, ln_b, o
                 regroup_matrix(step)
             if step == 0:
                 quantise_rows()
+                spread_residual_vectors()
             if step - QUANTISE_LAG in range(EXPERTS):
                 quantise_matrix(step - QUANTISE_LAG)
                 first_product(step - QUANTISE_LAG)
@@ -251,8 +261,6 @@ def tile_hdmodel_pb_s_kernel(tc, xs_mix, task_emb, W1, b1, W2, b2, ln_g, ln_b, o
                 add_bias(step - BIAS_LAG)
             if step - SILU_LAG in range(EXPERTS):
                 quantise_hidden(step - SILU_LAG)
-            if step == QUANTISE_LAG:
-                spread_residual_vectors()
             if step == BIAS_LAG + EXPERTS:
                 nc.vector.tensor_tensor(out=base[:], in0=add_rows[:], in1=x_mix[:], op=ALU.add)
 
@@ -270,11 +278,18 @@ def tile_hdmodel_pb_s_kernel(tc, xs_mix, task_emb, W1, b1, W2, b2, ln_g, ln_b, o
         std = keep.tile([ROWS, 1], F32)
         nc.scalar.activation(out=std[:], in_=mean_var[:, 1:2], func=ACT.Sqrt, bias=eps[:])
         centred = keep.tile([ROWS, WIDTH], F32)
-        nc.vector.scalar_tensor_tensor(
-            out=centred[:], in0=r[:], scalar=mean_var[:, 0:1], in1=gain_rows[:], op0=ALU.subtract, op1=ALU.mult
-        )
         rstd = keep.tile([ROWS, 1], F32)
-        nc.vector.reciprocal(out=rstd[:], in_=std[:])
+        for i, cols in enumerate(halves):
+            nc.vector.scalar_tensor_tensor(
+                out=centred[:, cols],
+                in0=r[:, cols],
+                scalar=mean_var[:, 0:1],
+                in1=gain_rows[:, cols],
+                op0=ALU.subtract,
+                op1=ALU.mult,
+            )
+            if i == 0:
+                nc.vector.reciprocal(out=rstd[:], in_=std[:])
         y = keep.tile([ROWS, WIDTH], F32)
         out_rows = out.flatten_outer_dims()
         for cols in halves:

@@ -21,13 +21,14 @@ CHUNKS = WIDTH // P
 HALF = WIDTH // 2
 MATRICES = 2 * EXPERTS
 EPS = 1e-5
+SEL_COLS = WIDTH - P
 
 ROW_TASK = 0
 ROW_B1 = ROW_TASK + TASKS
 ROW_B2 = ROW_B1 + EXPERTS
 SMALL_ROWS = ROW_B2 + EXPERTS
 
-VECTOR_COLS = 208
+VECTOR_COLS = 232
 FIRST_VECTOR_COLS = 128
 LAST_VECTOR_COLS = 64
 
@@ -68,6 +69,15 @@ def tile_hdmodel_pb_s_kernel(tc, xs_mix, task_emb, W1, b1, W2, b2, ln_g, ln_b, o
         nc.vector.memset(eps[:], EPS)
         h_grouped = keep.tile([P, EXPERTS, ROWS, PACK], BF16, align_bytes=64)
         nc.vector.memset(h_grouped[:].rearrange("q n r t -> q (n r t)").bitcast(F32), 0.0)
+
+        sel = keep.tile([P, ROWS], BF16)
+        row_dims = [P, BATCH, EXPERTS, TASKS]
+        nc.vector.tensor_tensor(
+            out=sel[:].rearrange("k (b n p) -> k b n p", b=BATCH, n=EXPERTS),
+            in0=ident[:, ROW_TASK : ROW_TASK + TASKS].unsqueeze(1).unsqueeze(1).to_broadcast(row_dims),
+            in1=ident[:, ROW_B2 : ROW_B2 + EXPERTS].unsqueeze(2).unsqueeze(1).to_broadcast(row_dims),
+            op=ALU.add,
+        )
 
         x_mix = keep.tile([ROWS, WIDTH], BF16)
         nc.sync.dma_start(out=x_mix[:], in_=xs_mix.flatten_outer_dims())
@@ -110,6 +120,9 @@ def tile_hdmodel_pb_s_kernel(tc, xs_mix, task_emb, W1, b1, W2, b2, ln_g, ln_b, o
         for c in range(CHUNKS):
             nc.tensor.transpose(small_t_psum[:, c, :], small[:, c * P : (c + 1) * P], ident[:])
 
+        add_rows = psum.tile([ROWS, WIDTH], F32)
+        nc.tensor.matmul(add_rows[:, 0:SEL_COLS], lhsT=sel[:], rhs=small[:, 0:SEL_COLS], start=True, stop=True)
+
         grouped_tiles = []
         codes_tiles = []
         scales_tiles = []
@@ -120,24 +133,21 @@ def tile_hdmodel_pb_s_kernel(tc, xs_mix, task_emb, W1, b1, W2, b2, ln_g, ln_b, o
         x_scales = keep.tile([P, ROWS], U8, align_bytes=64)
         h_codes = keep.tile([P, EXPERTS, ROWS], U32, align_bytes=64)
         h_scales = keep.tile([P, EXPERTS, ROWS], U8, align_bytes=64)
-        add_np = keep.tile([P, CHUNKS, EXPERTS, TASKS], F32)
-        add_rows = psum.tile([ROWS, WIDTH], F32)
+        add_np = keep.tile([P, EXPERTS, TASKS], F32)
         base = keep.tile([ROWS, WIDTH], F32)
         result = [psum.tile([ROWS, HALF], F32, name="result%d" % i) for i in range(len(halves))]
 
         def regroup_matrix(m):
             grouped = weights.tile([P, WIDTH, PACK], BF16, align_bytes=64)
             if m == 0:
-                scalar_cols = WIDTH - FIRST_VECTOR_COLS
-                for cols in (halves[0], slice(HALF, scalar_cols)):
-                    regroup(nc.scalar.copy, grouped, raw_tiles[m], cols)
-                regroup(nc.vector.tensor_copy, grouped, raw_tiles[m], slice(scalar_cols, WIDTH))
-                grouped_tiles.append(grouped)
-                return
-            last = m == MATRICES - 1
-            vector_cols = LAST_VECTOR_COLS if last else VECTOR_COLS
+                vector_cols = FIRST_VECTOR_COLS
+            elif m == MATRICES - 1:
+                vector_cols = LAST_VECTOR_COLS
+            else:
+                vector_cols = VECTOR_COLS
+            by_halves = m in (0, MATRICES - 1)
             regroup(nc.vector.tensor_copy, grouped, raw_tiles[m], slice(0, vector_cols))
-            for cols in [slice(vector_cols, HALF), halves[1]] if last else [slice(vector_cols, WIDTH)]:
+            for cols in [slice(vector_cols, HALF), halves[1]] if by_halves else [slice(vector_cols, WIDTH)]:
                 regroup(nc.scalar.copy, grouped, raw_tiles[m], cols)
             grouped_tiles.append(grouped)
 
@@ -169,8 +179,8 @@ def tile_hdmodel_pb_s_kernel(tc, xs_mix, task_emb, W1, b1, W2, b2, ln_g, ln_b, o
             nc.vector.tensor_copy(out=small_t[:], in_=small_t_psum[:, :, 0:SMALL_ROWS])
             nc.vector.tensor_tensor(
                 out=add_np[:],
-                in0=small_t[:, :, ROW_B2 : ROW_B2 + EXPERTS].unsqueeze(3).to_broadcast([P, CHUNKS, EXPERTS, TASKS]),
-                in1=small_t[:, :, ROW_TASK : ROW_TASK + TASKS].unsqueeze(2).to_broadcast([P, CHUNKS, EXPERTS, TASKS]),
+                in0=small_t[:, CHUNKS - 1, ROW_B2 : ROW_B2 + EXPERTS].unsqueeze(2).to_broadcast([P, EXPERTS, TASKS]),
+                in1=small_t[:, CHUNKS - 1, ROW_TASK : ROW_TASK + TASKS].unsqueeze(1).to_broadcast([P, EXPERTS, TASKS]),
                 op=ALU.add,
             )
             nc.vector.quantize_mx(
@@ -180,18 +190,12 @@ def tile_hdmodel_pb_s_kernel(tc, xs_mix, task_emb, W1, b1, W2, b2, ln_g, ln_b, o
             )
 
         def spread_residual_vectors():
-            add_t = keep.tile([P, CHUNKS, BATCH, ROWS_OF_B], F32)
+            add_t = keep.tile([P, BATCH, ROWS_OF_B], F32)
             nc.vector.tensor_copy(
                 out=add_t[:],
-                in_=add_np[:]
-                .rearrange("q c n p -> q c (n p)")
-                .unsqueeze(2)
-                .to_broadcast([P, CHUNKS, BATCH, ROWS_OF_B]),
+                in_=add_np[:].rearrange("q n p -> q (n p)").unsqueeze(1).to_broadcast([P, BATCH, ROWS_OF_B]),
             )
-            for c in range(CHUNKS):
-                nc.tensor.transpose(
-                    add_rows[:, c * P : (c + 1) * P], add_t[:, c].rearrange("q b r -> q (b r)"), ident_f32[:]
-                )
+            nc.tensor.transpose(add_rows[:, SEL_COLS:WIDTH], add_t[:].rearrange("q b r -> q (b r)"), ident_f32[:])
 
         def first_product(n):
             hidden = psum_hidden.tile([P, PACK, ROWS], F32)
@@ -243,6 +247,9 @@ def tile_hdmodel_pb_s_kernel(tc, xs_mix, task_emb, W1, b1, W2, b2, ln_g, ln_b, o
                     stop=(n == EXPERTS - 1),
                 )
 
+        def add_base(cols):
+            nc.vector.tensor_tensor(out=base[:, cols], in0=add_rows[:, cols], in1=x_mix[:, cols], op=ALU.add)
+
         for step in range(MATRICES + QUANTISE_LAG):
             if step - SILU_LAG in range(EXPERTS):
                 apply_silu(step - SILU_LAG)
@@ -262,11 +269,12 @@ def tile_hdmodel_pb_s_kernel(tc, xs_mix, task_emb, W1, b1, W2, b2, ln_g, ln_b, o
             if step - SILU_LAG in range(EXPERTS):
                 quantise_hidden(step - SILU_LAG)
             if step == BIAS_LAG + EXPERTS:
-                nc.vector.tensor_tensor(out=base[:], in0=add_rows[:], in1=x_mix[:], op=ALU.add)
+                add_base(halves[0])
 
         warm_sqrt = keep.tile([P, 1], F32)
         nc.scalar.activation(out=warm_sqrt[:], in_=one[:], func=ACT.Sqrt)
 
+        add_base(halves[1])
         r = keep.tile([ROWS, WIDTH], F32)
         stats = keep.tile([ROWS, len(halves), 6], F32)
         for i, cols in enumerate(halves):

@@ -10,6 +10,7 @@ ALU = mybir.AluOpType
 ACT = mybir.ActivationFunctionType
 
 P = 128
+RUN = 2
 PACK = 4
 BATCH = 4
 EXPERTS = 4
@@ -41,8 +42,8 @@ FLOPS = 2 * 2 * ROWS * WIDTH * WIDTH
 
 def regroup(engine_copy, grouped, raw, cols):
     engine_copy(
-        out=grouped[:, cols, :].rearrange("q (c i) j -> q c j i", i=4),
-        in_=raw[:, :, cols].rearrange("q j (c i) -> q c j i", i=4),
+        out=grouped[:, cols, :].rearrange("q (c i) j -> q c j i", i=RUN),
+        in_=raw[:, :, cols].rearrange("q j (c i) -> q c j i", i=RUN),
     )
 
 

@@ -84,13 +84,21 @@ def tile_hdmodel_pb_s_kernel(tc, xs_mix, task_emb, W1, b1, W2, b2, ln_g, ln_b, o
         nc.sync.dma_start(out=x_mix[:], in_=xs_mix.flatten_outer_dims())
         raw_tiles = []
         for n in range(EXPERTS):
+            source = W1[n].rearrange("(q j) w -> q j w", j=PACK)
+            if n == 0:
+                first_halves = []
+                for cols in halves:
+                    raw_half = keep.tile([P, PACK, HALF], BF16, name="raw_half%d" % len(first_halves))
+                    nc.sync.dma_start(out=raw_half[:], in_=source[:, :, cols])
+                    first_halves.append(raw_half)
+                    if cols == halves[0]:
+                        nc.sync.dma_start(out=small[ROW_TASK : ROW_TASK + TASKS, :], in_=task_emb)
+                        nc.sync.dma_start(out=small[ROW_B1 : ROW_B1 + EXPERTS, :], in_=b1)
+                        nc.sync.dma_start(out=small[ROW_B2 : ROW_B2 + EXPERTS, :], in_=b2)
+                raw_tiles.append(None)
+                continue
             raw = weights.tile([P, PACK, WIDTH], BF16)
-            for cols in halves if n == 0 else [slice(0, WIDTH)]:
-                nc.sync.dma_start(out=raw[:, :, cols], in_=W1[n].rearrange("(q j) w -> q j w", j=PACK)[:, :, cols])
-                if cols == halves[0]:
-                    nc.sync.dma_start(out=small[ROW_TASK : ROW_TASK + TASKS, :], in_=task_emb)
-                    nc.sync.dma_start(out=small[ROW_B1 : ROW_B1 + EXPERTS, :], in_=b1)
-                    nc.sync.dma_start(out=small[ROW_B2 : ROW_B2 + EXPERTS, :], in_=b2)
+            nc.sync.dma_start(out=raw[:], in_=source)
             raw_tiles.append(raw)
         for n in range(EXPERTS):
             raw = weights.tile([P, PACK, WIDTH], BF16)
@@ -140,17 +148,18 @@ def tile_hdmodel_pb_s_kernel(tc, xs_mix, task_emb, W1, b1, W2, b2, ln_g, ln_b, o
 
         def regroup_matrix(m):
             grouped = weights.tile([P, WIDTH, PACK], BF16, align_bytes=64)
-            if m == 0:
-                vector_cols = FIRST_VECTOR_COLS
-            elif m == MATRICES - 1:
-                vector_cols = LAST_VECTOR_COLS
-            else:
-                vector_cols = VECTOR_COLS
-            by_halves = m in (0, MATRICES - 1)
-            regroup(nc.vector.tensor_copy, grouped, raw_tiles[m], slice(0, vector_cols))
-            for cols in [slice(vector_cols, HALF), halves[1]] if by_halves else [slice(vector_cols, WIDTH)]:
-                regroup(nc.scalar.copy, grouped, raw_tiles[m], cols)
             grouped_tiles.append(grouped)
+            if m == 0:
+                first, second = [grouped[:, cols, :] for cols in halves]
+                regroup(nc.vector.tensor_copy, first, first_halves[0], slice(0, FIRST_VECTOR_COLS))
+                regroup(nc.scalar.copy, first, first_halves[0], slice(FIRST_VECTOR_COLS, HALF))
+                regroup(nc.scalar.copy, second, first_halves[1], slice(0, HALF))
+                return
+            last = m == MATRICES - 1
+            vector_cols = LAST_VECTOR_COLS if last else VECTOR_COLS
+            regroup(nc.vector.tensor_copy, grouped, raw_tiles[m], slice(0, vector_cols))
+            for cols in [slice(vector_cols, HALF), halves[1]] if last else [slice(vector_cols, WIDTH)]:
+                regroup(nc.scalar.copy, grouped, raw_tiles[m], cols)
 
         def quantise_matrix(m):
             w_codes = weights.tile([P, WIDTH], U32, align_bytes=64)

@@ -22,7 +22,7 @@ CHUNKS = WIDTH // P
 HALF = WIDTH // 2
 MATRICES = 2 * EXPERTS
 EPS = 1e-5
-SEL_COLS = WIDTH - P
+SEL_PLANES = PACK - 1
 
 ROW_TASK = 0
 ROW_B1 = ROW_TASK + TASKS
@@ -130,14 +130,22 @@ def tile_hdmodel_pb_s_kernel(tc, xs_mix, task_emb, W1, b1, W2, b2, ln_g, ln_b, o
             nc.tensor.transpose(small_t_psum[:, c, :], small[:, c * P : (c + 1) * P], ident[:])
 
         add_rows = psum.tile([ROWS, WIDTH], F32)
-        nc.tensor.matmul(add_rows[:, 0:SEL_COLS], lhsT=sel[:], rhs=small[:, 0:SEL_COLS], start=True, stop=True)
+        add_rows_by_j = add_rows[:].rearrange("r (q j) -> r q j", j=PACK)
+        nc.tensor.matmul(
+            add_rows_by_j[:, :, 0:SEL_PLANES],
+            lhsT=sel[:],
+            rhs=small[:].rearrange("k (q j) -> k q j", j=PACK)[:, :, 0:SEL_PLANES],
+            start=True,
+            stop=True,
+        )
 
         grouped_tiles = []
         codes_tiles = []
         scales_tiles = []
         hidden_tiles = []
         biased_tiles = []
-        small_t = keep.tile([P, CHUNKS, SMALL_ROWS], BF16)
+        small_t = keep.tile([P, PACK, SMALL_ROWS], BF16)
+        b1_t = keep.tile([P, CHUNKS, EXPERTS], BF16)
         x_codes = keep.tile([P, ROWS], U32, align_bytes=64)
         x_scales = keep.tile([P, ROWS], U8, align_bytes=64)
         h_codes = keep.tile([P, EXPERTS, ROWS], U32, align_bytes=64)
@@ -174,23 +182,22 @@ def tile_hdmodel_pb_s_kernel(tc, xs_mix, task_emb, W1, b1, W2, b2, ln_g, ln_b, o
             scales_tiles.append(w_scales)
 
         def quantise_rows():
-            task_t_packed = keep.tile([P, PACK, TASKS], BF16)
-            nc.vector.tensor_copy(out=task_t_packed[:], in_=small_t_packed[:, :, ROW_TASK : ROW_TASK + TASKS])
+            nc.vector.tensor_copy(out=small_t[:], in_=small_t_packed[:, :, 0:SMALL_ROWS])
+            nc.scalar.copy(out=b1_t[:], in_=small_t_psum[:, :, ROW_B1 : ROW_B1 + EXPERTS])
             x_grouped = keep.tile([P, ROWS, PACK], BF16, align_bytes=64)
             nc.vector.tensor_tensor(
                 out=x_grouped[:].rearrange("q (a p) j -> q a p j", p=TASKS),
                 in0=x_t[:].rearrange("q j (a p) -> q a p j", p=TASKS),
-                in1=task_t_packed[:]
+                in1=small_t[:, :, ROW_TASK : ROW_TASK + TASKS]
                 .rearrange("q j p -> q p j")
                 .unsqueeze(1)
                 .to_broadcast([P, BATCH * EXPERTS, TASKS, PACK]),
                 op=ALU.add,
             )
-            nc.vector.tensor_copy(out=small_t[:], in_=small_t_psum[:, :, 0:SMALL_ROWS])
             nc.vector.tensor_tensor(
                 out=add_np[:],
-                in0=small_t[:, CHUNKS - 1, ROW_B2 : ROW_B2 + EXPERTS].unsqueeze(2).to_broadcast([P, EXPERTS, TASKS]),
-                in1=small_t[:, CHUNKS - 1, ROW_TASK : ROW_TASK + TASKS].unsqueeze(1).to_broadcast([P, EXPERTS, TASKS]),
+                in0=small_t[:, SEL_PLANES, ROW_B2 : ROW_B2 + EXPERTS].unsqueeze(2).to_broadcast([P, EXPERTS, TASKS]),
+                in1=small_t[:, SEL_PLANES, ROW_TASK : ROW_TASK + TASKS].unsqueeze(1).to_broadcast([P, EXPERTS, TASKS]),
                 op=ALU.add,
             )
             nc.vector.quantize_mx(
@@ -205,7 +212,9 @@ def tile_hdmodel_pb_s_kernel(tc, xs_mix, task_emb, W1, b1, W2, b2, ln_g, ln_b, o
                 out=add_t[:],
                 in_=add_np[:].rearrange("q n p -> q (n p)").unsqueeze(1).to_broadcast([P, BATCH, ROWS_OF_B]),
             )
-            nc.tensor.transpose(add_rows[:, SEL_COLS:WIDTH], add_t[:].rearrange("q b r -> q (b r)"), ident_f32[:])
+            nc.tensor.transpose(
+                add_rows_by_j[:, :, SEL_PLANES], add_t[:].rearrange("q b r -> q (b r)"), ident_f32[:]
+            )
 
         def first_product(n):
             hidden = psum_hidden.tile([P, PACK, ROWS], F32)
@@ -226,7 +235,7 @@ def tile_hdmodel_pb_s_kernel(tc, xs_mix, task_emb, W1, b1, W2, b2, ln_g, ln_b, o
             nc.vector.tensor_tensor(
                 out=biased[:],
                 in0=hidden_tiles[n][:].rearrange("q t (b e p) -> q t b e p", b=BATCH, e=EXPERTS)[:, :, :, n, :],
-                in1=small_t[:, :, ROW_B1 + n].unsqueeze(2).unsqueeze(3).to_broadcast([P, PACK, BATCH, TASKS]),
+                in1=b1_t[:, :, n].unsqueeze(2).unsqueeze(3).to_broadcast([P, PACK, BATCH, TASKS]),
                 op=ALU.add,
             )
             biased_tiles.append(biased)

import concourse.mybir as mybir
from concourse.masks import make_identity

F32 = mybir.dt.float32
BF16 = mybir.dt.bfloat16
U32 = mybir.dt.uint32
U8 = mybir.dt.uint8
FP8X4 = mybir.dt.float8_e4m3fn_x4
ALU = mybir.AluOpType
ACT = mybir.ActivationFunctionType

P = 128
RUN = 2
PACK = 4
BATCH = 4
EXPERTS = 4
TASKS = 8
ROWS = BATCH * EXPERTS * TASKS
ROWS_OF_B = EXPERTS * TASKS
WIDTH = 512
CHUNKS = WIDTH // P
HALF = WIDTH // 2
MATRICES = 2 * EXPERTS
EPS = 1e-5
SEL_PLANES = PACK - 1

ROW_TASK = 0
ROW_B1 = ROW_TASK + TASKS
ROW_B2 = ROW_B1 + EXPERTS
SMALL_ROWS = ROW_B2 + EXPERTS

VECTOR_COLS = 232
FIRST_VECTOR_COLS = 128
LAST_VECTOR_COLS = 64

QUANTISE_LAG = 1
BIAS_LAG = 2
SILU_LAG = 4

FLOPS = 2 * 2 * ROWS * WIDTH * WIDTH


def regroup(engine_copy, grouped, raw, cols):
    engine_copy(
        out=grouped[:, cols, :].rearrange("q (c i) j -> q c j i", i=RUN),
        in_=raw[:, :, cols].rearrange("q j (c i) -> q c j i", i=RUN),
    )


def tile_hdmodel_pb_s_kernel(tc, xs_mix, task_emb, W1, b1, W2, b2, ln_g, ln_b, out):
    nc = tc.nc
    halves = [slice(0, HALF), slice(HALF, WIDTH)]
    with (
        tc.tile_pool(name="keep", bufs=1) as keep,
        tc.tile_pool(name="weights", bufs=MATRICES) as weights,
        tc.tile_pool(name="experts", bufs=EXPERTS) as experts,
        tc.psum_pool(name="psum", bufs=1) as psum,
        tc.psum_pool(name="psum_hidden", bufs=2) as psum_hidden,
        tc.manual_schedule(),
    ):
        small = keep.tile([P, WIDTH], BF16)
        nc.vector.memset(small[:].bitcast(F32), 0.0)
        ident = keep.tile([P, P], BF16)
        make_identity(nc, ident[:])
        ident_f32 = keep.tile([P, P], F32)
        make_identity(nc, ident_f32[:])
        one = keep.tile([P, 1], F32)
        nc.vector.memset(one[:], 1.0)
        eps = keep.tile([P, 1], F32)
        nc.vector.memset(eps[:], EPS)
        h_grouped = keep.tile([P, EXPERTS, ROWS, PACK], BF16, align_bytes=64)
        nc.vector.memset(h_grouped[:].rearrange("q n r t -> q (n r t)").bitcast(F32), 0.0)

        sel = keep.tile([P, ROWS], BF16)
        row_dims = [P, BATCH, EXPERTS, TASKS]
        nc.vector.tensor_tensor(
            out=sel[:].rearrange("k (b n p) -> k b n p", b=BATCH, n=EXPERTS),
            in0=ident[:, ROW_TASK : ROW_TASK + TASKS].unsqueeze(1).unsqueeze(1).to_broadcast(row_dims),
            in1=ident[:, ROW_B2 : ROW_B2 + EXPERTS].unsqueeze(2).unsqueeze(1).to_broadcast(row_dims),
            op=ALU.add,
        )

        x_mix = keep.tile([ROWS, WIDTH], BF16)
        nc.sync.dma_start(out=x_mix[:], in_=xs_mix.flatten_outer_dims())
        raw_tiles = []
        for n in range(EXPERTS):
            source = W1[n].rearrange("(q j) w -> q j w", j=PACK)
            if n == 0:
                first_halves = []
                for cols in halves:
                    raw_half = keep.tile([P, PACK, HALF], BF16, name="raw_half%d" % len(first_halves))
                    nc.sync.dma_start(out=raw_half[:], in_=source[:, :, cols])
                    first_halves.append(raw_half)
                    if cols == halves[0]:
                        nc.sync.dma_start(out=small[ROW_TASK : ROW_TASK + TASKS, :], in_=task_emb)
                        nc.sync.dma_start(out=small[ROW_B1 : ROW_B1 + EXPERTS, :], in_=b1)
                        nc.sync.dma_start(out=small[ROW_B2 : ROW_B2 + EXPERTS, :], in_=b2)
                raw_tiles.append(None)
                continue
            raw = weights.tile([P, PACK, WIDTH], BF16)
            nc.sync.dma_start(out=raw[:], in_=source)
            raw_tiles.append(raw)
        for n in range(EXPERTS):
            raw = weights.tile([P, PACK, WIDTH], BF16)
            nc.sync.dma_start(out=raw[:], in_=W2[n].rearrange("(t q) w -> q t w", q=P))
            raw_tiles.append(raw)
        norm_rows = []
        for vector in (ln_g, ln_b):
            rows_tile = keep.tile([ROWS, WIDTH], BF16, name="norm_rows%d" % len(norm_rows))
            for b in range(BATCH):
                nc.sync.dma_start(
                    out=rows_tile[b * ROWS_OF_B : (b + 1) * ROWS_OF_B, :],
                    in_=vector.unsqueeze(1).to_broadcast([EXPERTS, TASKS, WIDTH]),
                )
            norm_rows.append(rows_tile)
        gain_rows, shift_rows = norm_rows

        warm_silu = keep.tile([P, 1], F32)
        nc.scalar.activation(out=warm_silu[:], in_=one[:], func=ACT.Silu)

        x_t = psum.tile([P, PACK, ROWS], BF16)
        small_t_packed = psum.tile([P, PACK, P], BF16)
        for source, target in ((x_mix, x_t), (small, small_t_packed)):
            for j in range(PACK):
                nc.tensor.transpose(
                    target[:, j, :], source[:].rearrange("r (q j) -> r j q", j=PACK)[:, j, :], ident[:]
                )
        small_t_psum = psum.tile([P, CHUNKS, P], BF16)
        for c in range(CHUNKS):
            nc.tensor.transpose(small_t_psum[:, c, :], small[:, c * P : (c + 1) * P], ident[:])

        add_rows = psum.tile([ROWS, WIDTH], F32)
        add_rows_by_j = add_rows[:].rearrange("r (q j) -> r q j", j=PACK)
        nc.tensor.matmul(
            add_rows_by_j[:, :, 0:SEL_PLANES],
            lhsT=sel[:],
            rhs=small[:].rearrange("k (q j) -> k q j", j=PACK)[:, :, 0:SEL_PLANES],
            start=True,
            stop=True,
        )

        grouped_tiles = []
        codes_tiles = []
        scales_tiles = []
        hidden_tiles = []
        biased_tiles = []
        small_t = keep.tile([P, PACK, SMALL_ROWS], BF16)
        b1_t = keep.tile([P, CHUNKS, EXPERTS], BF16)
        x_codes = keep.tile([P, ROWS], U32, align_bytes=64)
        x_scales = keep.tile([P, ROWS], U8, align_bytes=64)
        h_codes = keep.tile([P, EXPERTS, ROWS], U32, align_bytes=64)
        h_scales = keep.tile([P, EXPERTS, ROWS], U8, align_bytes=64)
        add_np = keep.tile([P, EXPERTS, TASKS], F32)
        base = keep.tile([ROWS, WIDTH], F32)
        result = [psum.tile([ROWS, HALF], F32, name="result%d" % i) for i in range(len(halves))]

        def regroup_matrix(m):
            grouped = weights.tile([P, WIDTH, PACK], BF16, align_bytes=64)
            grouped_tiles.append(grouped)
            if m == 0:
                first, second = [grouped[:, cols, :] for cols in halves]
                regroup(nc.vector.tensor_copy, first, first_halves[0], slice(0, FIRST_VECTOR_COLS))
                regroup(nc.scalar.copy, first, first_halves[0], slice(FIRST_VECTOR_COLS, HALF))
                regroup(nc.scalar.copy, second, first_halves[1], slice(0, HALF))
                return
            last = m == MATRICES - 1
            vector_cols = LAST_VECTOR_COLS if last else VECTOR_COLS
            regroup(nc.vector.tensor_copy, grouped, raw_tiles[m], slice(0, vector_cols))
            for cols in [slice(vector_cols, HALF), halves[1]] if last else [slice(vector_cols, WIDTH)]:
                regroup(nc.scalar.copy, grouped, raw_tiles[m], cols)

        def quantise_matrix(m):
            w_codes = weights.tile([P, WIDTH], U32, align_bytes=64)
            w_scales = weights.tile([P, WIDTH], U8, align_bytes=64)
            for cols in halves if m == MATRICES - 1 else [slice(0, WIDTH)]:
                nc.vector.quantize_mx(
                    out=w_codes[:, cols].bitcast(FP8X4),
                    scales=w_scales[:, cols],
                    in_=grouped_tiles[m][:, cols, :].rearrange("q w j -> q (w j)"),
                )
            codes_tiles.append(w_codes)
            scales_tiles.append(w_scales)

        def quantise_rows():
            nc.vector.tensor_copy(out=small_t[:], in_=small_t_packed[:, :, 0:SMALL_ROWS])
            nc.scalar.copy(out=b1_t[:], in_=small_t_psum[:, :, ROW_B1 : ROW_B1 + EXPERTS])
            x_grouped = keep.tile([P, ROWS, PACK], BF16, align_bytes=64)
            nc.vector.tensor_tensor(
                out=x_grouped[:].rearrange("q (a p) j -> q a p j", p=TASKS),
                in0=x_t[:].rearrange("q j (a p) -> q a p j", p=TASKS),
                in1=small_t[:, :, ROW_TASK : ROW_TASK + TASKS]
                .rearrange("q j p -> q p j")
                .unsqueeze(1)
                .to_broadcast([P, BATCH * EXPERTS, TASKS, PACK]),
                op=ALU.add,
            )
            nc.vector.tensor_tensor(
                out=add_np[:],
                in0=small_t[:, SEL_PLANES, ROW_B2 : ROW_B2 + EXPERTS].unsqueeze(2).to_broadcast([P, EXPERTS, TASKS]),
                in1=small_t[:, SEL_PLANES, ROW_TASK : ROW_TASK + TASKS].unsqueeze(1).to_broadcast([P, EXPERTS, TASKS]),
                op=ALU.add,
            )
            nc.vector.quantize_mx(
                out=x_codes[:].bitcast(FP8X4),
                scales=x_scales[:],
                in_=x_grouped[:].rearrange("q r j -> q (r j)"),
            )

        def spread_residual_vectors():
            add_t = keep.tile([P, BATCH, ROWS_OF_B], F32)
            nc.vector.tensor_copy(
                out=add_t[:],
                in_=add_np[:].rearrange("q n p -> q (n p)").unsqueeze(1).to_broadcast([P, BATCH, ROWS_OF_B]),
            )
            nc.tensor.transpose(
                add_rows_by_j[:, :, SEL_PLANES], add_t[:].rearrange("q b r -> q (b r)"), ident_f32[:]
            )

        def first_product(n):
            hidden = psum_hidden.tile([P, PACK, ROWS], F32)
            for t in range(PACK):
                nc.tensor.matmul_mx(
                    out=hidden[:, t, :],
                    lhsT=codes_tiles[n][:, t * P : (t + 1) * P].bitcast(FP8X4),
                    lhsT_scale=scales_tiles[n][:, t * P : (t + 1) * P],
                    rhs=x_codes[:].bitcast(FP8X4),
                    rhs_scale=x_scales[:],
                    start=True,
                    stop=True,
                )
            hidden_tiles.append(hidden)

        def add_bias(n):
            biased = experts.tile([P, PACK, BATCH, TASKS], F32)
            nc.vector.tensor_tensor(
                out=biased[:],
                in0=hidden_tiles[n][:].rearrange("q t (b e p) -> q t b e p", b=BATCH, e=EXPERTS)[:, :, :, n, :],
                in1=b1_t[:, :, n].unsqueeze(2).unsqueeze(3).to_broadcast([P, PACK, BATCH, TASKS]),
                op=ALU.add,
            )
            biased_tiles.append(biased)

        def apply_silu(n):
            nc.scalar.activation(
                out=h_grouped[:, n].rearrange("q (b e p) t -> q b e p t", b=BATCH, e=EXPERTS)[:, :, n, :, :],
                in_=biased_tiles[n][:].rearrange("q t b p -> q b p t"),
                func=ACT.Silu,
            )

        def quantise_hidden(n):
            nc.vector.quantize_mx(
                out=h_codes[:, n, :].bitcast(FP8X4),
                scales=h_scales[:, n, :],
                in_=h_grouped[:, n].rearrange("q r t -> q (r t)"),
            )

        def second_product(n):
            for i, cols in enumerate(halves):
                nc.tensor.matmul_mx(
                    out=result[i][:],
                    lhsT=h_codes[:, n, :].bitcast(FP8X4),
                    lhsT_scale=h_scales[:, n, :],
                    rhs=codes_tiles[EXPERTS + n][:, cols].bitcast(FP8X4),
                    rhs_scale=scales_tiles[EXPERTS + n][:, cols],
                    start=(n == 0),
                    stop=(n == EXPERTS - 1),
                )

        def add_base(cols):
            nc.vector.tensor_tensor(out=base[:, cols], in0=add_rows[:, cols], in1=x_mix[:, cols], op=ALU.add)

        for step in range(MATRICES + QUANTISE_LAG):
            if step - SILU_LAG in range(EXPERTS):
                apply_silu(step - SILU_LAG)
            if step in range(MATRICES):
                regroup_matrix(step)
            if step == 0:
                quantise_rows()
                spread_residual_vectors()
            if step - QUANTISE_LAG in range(EXPERTS):
                quantise_matrix(step - QUANTISE_LAG)
                first_product(step - QUANTISE_LAG)
            if step - QUANTISE_LAG in range(EXPERTS, MATRICES):
                quantise_matrix(step - QUANTISE_LAG)
                second_product(step - QUANTISE_LAG - EXPERTS)
            if step - BIAS_LAG in range(EXPERTS):
                add_bias(step - BIAS_LAG)
            if step - SILU_LAG in range(EXPERTS):
                quantise_hidden(step - SILU_LAG)
            if step == BIAS_LAG + EXPERTS:
                add_base(halves[0])

        warm_sqrt = keep.tile([P, 1], F32)
        nc.scalar.activation(out=warm_sqrt[:], in_=one[:], func=ACT.Sqrt)

        add_base(halves[1])
        r = keep.tile([ROWS, WIDTH], F32)
        stats = keep.tile([ROWS, len(halves), 6], F32)
        for i, cols in enumerate(halves):
            nc.vector.tensor_tensor(out=r[:, cols], in0=result[i][:], in1=base[:, cols], op=ALU.add)
        for i, cols in enumerate(halves):
            nc.vector.bn_stats(out=stats[:, i, :], in_=r[:, cols])
        mean_var = keep.tile([ROWS, 2], F32)
        nc.vector.bn_aggr(out=mean_var[:], in_=stats[:].rearrange("r i s -> r (i s)"))
        std = keep.tile([ROWS, 1], F32)
        nc.scalar.activation(out=std[:], in_=mean_var[:, 1:2], func=ACT.Sqrt, bias=eps[:])
        centred = keep.tile([ROWS, WIDTH], F32)
        rstd = keep.tile([ROWS, 1], F32)
        for i, cols in enumerate(halves):
            nc.vector.scalar_tensor_tensor(
                out=centred[:, cols],
                in0=r[:, cols],
                scalar=mean_var[:, 0:1],
                in1=gain_rows[:, cols],
                op0=ALU.subtract,
                op1=ALU.mult,
            )
            if i == 0:
                nc.vector.reciprocal(out=rstd[:], in_=std[:])
        y = keep.tile([ROWS, WIDTH], F32)
        out_rows = out.flatten_outer_dims()
        for cols in halves:
            nc.vector.scalar_tensor_tensor(
                out=y[:, cols],
                in0=centred[:, cols],
                scalar=rstd[:],
                in1=shift_rows[:, cols],
                op0=ALU.mult,
                op1=ALU.add,
            )
            nc.sync.dma_start(out=out_rows[:, cols], in_=y[:, cols])
